import numpy as np
import ml_dtypes


def mxq(x, axis, fmt="e4m3"):
    dtype, down = {"e4m3": (ml_dtypes.float8_e4m3fn, 7), "e5m2": (ml_dtypes.float8_e5m2, 14)}[fmt]
    v = np.moveaxis(np.asarray(x, np.float32).astype(ml_dtypes.bfloat16).astype(np.float64), axis, -1)
    blocks = v.reshape(v.shape[:-1] + (-1, 32))
    amax = np.abs(blocks).max(-1, keepdims=True)
    byte = np.maximum(np.where(amax > 0, np.frexp(amax)[1] - 1 + 127, 0) - down, 1)
    scale = np.exp2(byte - 127.0)
    codes = (blocks / scale).astype(np.float32).astype(dtype).astype(np.float64)
    return np.moveaxis((codes * scale).reshape(v.shape), -1, axis)


WIDE = False


def mx_kscale(k):
    if not WIDE:
        return np.ones(k)
    levels = np.array([10, -10, 5, -5, 0])
    a = np.random.permutation(np.resize(levels, k // 512 * 4)).reshape(k // 512, 4)
    idx = np.arange(k)
    return np.exp2(a[idx // 512, idx % 128 // 32])


BF16 = ml_dtypes.bfloat16


def bf(x):
    return np.asarray(x, np.float32).astype(BF16)


def f64(x):
    return np.asarray(x).astype(np.float64)


E2M1 = np.array([0.0, 0.5, 1.0, 1.5, 2.0, 3.0, 4.0, 6.0, -0.0, -0.5, -1.0, -1.5, -2.0, -3.0, -4.0, -6.0])


def pack_weight(w, fmt):
    k, n = w.shape
    w = f64(bf(w)).reshape(k // 32, 32, n)
    amax = np.abs(w).max(1)
    if fmt == "e4m3":
        byte = np.frexp(amax)[1] - 1 + 127 - 7
    else:
        mant, ex = np.frexp(amax / 6.0)
        byte = np.where(mant > 0.5, ex, ex - 1) + 127
    byte = np.clip(np.where(amax > 0, byte, 1), 1, 254)
    scaled = (w * np.exp2(127.0 - byte)[:, None, :]).reshape(k, n).astype(np.float32)
    by_word = np.ascontiguousarray(scaled.reshape(k // 512, 128, 4, n).transpose(0, 1, 3, 2))
    if fmt == "e4m3":
        words = by_word.astype(ml_dtypes.float8_e4m3fn).view(np.uint8)
    else:
        c = by_word.astype(ml_dtypes.float4_e2m1fn).view(np.uint8) & 0xF
        words = c[..., 0::2] | (c[..., 1::2] << 4)
    return np.ascontiguousarray(words), np.ascontiguousarray(byte.astype(np.uint8).reshape(k // 512, 16, n))


def unpack_weight(words, scales, fmt):
    g, p, n, _ = words.shape
    if fmt == "e4m3":
        vals = np.ascontiguousarray(words).view(ml_dtypes.float8_e4m3fn).astype(np.float64)
    else:
        nib = np.empty((g, p, n, 4), np.uint8)
        nib[..., 0::2] = words & 0xF
        nib[..., 1::2] = words >> 4
        vals = E2M1[nib]
    vals = vals * np.repeat(np.exp2(scales.astype(np.float64) - 127.0), 8, axis=1)[..., None]
    return vals.transpose(0, 1, 3, 2).reshape(g * 512, n)

def pack4(w):
    words, scales = pack_weight(w, "e2m1")
    return words.reshape(words.shape[0], 128, -1), scales


def unpack4(words, scales):
    return unpack_weight(words.reshape(words.shape[0], 128, -1, 2), scales, "e2m1")


B, IN, H = 4096, 512, 512


def sigmoid(v):
    return 1.0 / (1.0 + np.exp(-v))


def setup_inputs():
    s, t = mx_kscale(IN), mx_kscale(H)
    a = np.sqrt(2.0 / (IN + H))
    x = bf(np.random.standard_normal((B, IN)) * s)
    h_prev = bf(np.random.standard_normal((B, H)) * t)
    m_prev = bf(np.random.standard_normal((B, H)) * 0.5)
    Wi_x_words, Wi_x_scales = pack4((np.random.standard_normal((H, IN)) * a / s).T)
    b_i = bf(np.random.standard_normal(H) * 0.3)
    Wi_h_words, Wi_h_scales = pack4((np.random.standard_normal((H, H)) * a / t).T)
    Wf_x_words, Wf_x_scales = pack4((np.random.standard_normal((H, IN)) * a / s).T)
    b_f = bf(2.0 + np.random.standard_normal(H) * 0.3)
    Wf_h_words, Wf_h_scales = pack4((np.random.standard_normal((H, H)) * a / t).T)
    return {
        "x": x,
        "h_prev": h_prev,
        "m_prev": m_prev,
        "Wi_x_words": Wi_x_words,
        "Wi_x_scales": Wi_x_scales,
        "b_i": b_i,
        "Wi_h_words": Wi_h_words,
        "Wi_h_scales": Wi_h_scales,
        "Wf_x_words": Wf_x_words,
        "Wf_x_scales": Wf_x_scales,
        "b_f": b_f,
        "Wf_h_words": Wf_h_words,
        "Wf_h_scales": Wf_h_scales,
    }


def reference(x, h_prev, m_prev, Wi_x_words, Wi_x_scales, b_i, Wi_h_words, Wi_h_scales, Wf_x_words, Wf_x_scales, b_f, Wf_h_words, Wf_h_scales):
    xq = mxq(f64(x), 1, "e4m3")
    hq = mxq(f64(h_prev), 1, "e4m3")
    i_tilde = (xq @ unpack4(Wi_x_words, Wi_x_scales)) + f64(b_i) + (hq @ unpack4(Wi_h_words, Wi_h_scales))
    f_aff = (xq @ unpack4(Wf_x_words, Wf_x_scales)) + f64(b_f) + (hq @ unpack4(Wf_h_words, Wf_h_scales))
    log_f = np.log(np.maximum(sigmoid(f_aff), 1e-8))
    m_t = np.maximum(log_f + f64(m_prev), i_tilde)
    i_prime = np.exp(i_tilde - m_t)
    f_prime = np.exp(log_f + f64(m_prev) - m_t)
    return m_t, i_prime, f_prime

@@ -1,0 +1,272 @@
+from contextlib import ExitStack
+
+import concourse.mybir as mybir
+from concourse.masks import make_identity
+
+F32 = mybir.dt.float32
+BF16 = mybir.dt.bfloat16
+I32 = mybir.dt.int32
+U32 = mybir.dt.uint32
+U8 = mybir.dt.uint8
+FP8X4 = mybir.dt.float8_e4m3fn_x4
+FP4X4 = mybir.dt.float4_e2m1fn_x4
+ALU = mybir.AluOpType
+ACT = mybir.ActivationFunctionType
+
+P = 128
+BATCH = 4096
+FEAT = 512
+ROW_TILES = 4
+UNIT_ROWS = P * ROW_TILES
+N_UNITS = BATCH // UNIT_ROWS
+OUT_CHUNKS = FEAT // P
+WORDS = FEAT // 2
+
+FLOPS = 2 * BATCH * FEAT * FEAT * 4
+
+
+def tile_slstmlayer_pa_t_kernel(
+    tc,
+    x,
+    h_prev,
+    m_prev,
+    Wi_x_words,
+    Wi_x_scales,
+    b_i,
+    Wi_h_words,
+    Wi_h_scales,
+    Wf_x_words,
+    Wf_x_scales,
+    b_f,
+    Wf_h_words,
+    Wf_h_scales,
+    out_0,
+    out_1,
+    out_2,
+):
+    nc = tc.nc
+    with ExitStack() as stack:
+        keep = stack.enter_context(tc.tile_pool(name="keep", bufs=1))
+        loads = stack.enter_context(tc.tile_pool(name="loads", bufs=3))
+        regroup = stack.enter_context(tc.tile_pool(name="regroup", bufs=2))
+        quant = stack.enter_context(tc.tile_pool(name="quant", bufs=3))
+        work = stack.enter_context(tc.tile_pool(name="work", bufs=3))
+        short = stack.enter_context(tc.tile_pool(name="short", bufs=2))
+        turn = stack.enter_context(tc.psum_pool(name="turn", bufs=4))
+        sums = stack.enter_context(tc.psum_pool(name="sums", bufs=4))
+        stack.enter_context(tc.manual_schedule())
+
+        def unit_view(tensor, u):
+            rows = tensor[u * UNIT_ROWS : (u + 1) * UNIT_ROWS, :]
+            return rows.rearrange("(p j) n -> p j n", j=ROW_TILES)
+
+        ident_f32 = keep.tile([P, P], F32, name="ident_f32")
+        make_identity(nc, ident_f32[:])
+        ident_bf16 = keep.tile([P, P], BF16, name="ident_bf16")
+        make_identity(nc, ident_bf16[:])
+
+        weight_names = ("f_x", "f_h", "i_x", "i_h")
+        weight_words = {"f_x": Wf_x_words, "f_h": Wf_h_words, "i_x": Wi_x_words, "i_h": Wi_h_words}
+        weight_scales = {"f_x": Wf_x_scales, "f_h": Wf_h_scales, "i_x": Wi_x_scales, "i_h": Wi_h_scales}
+        planes = keep.tile([P, len(weight_names), FEAT], U8, name="planes", align_bytes=64)
+        nc.vector.memset(planes[:].rearrange("p w n -> p (w n)").bitcast(I32), 0)
+        bf_rows = keep.tile([P, P], BF16, name="bf_rows")
+        nc.vector.memset(bf_rows[:], 0.0)
+        bi_row = keep.tile([P, FEAT], BF16, name="bi_row")
+        nc.vector.memset(bi_row[:], 0.0)
+        ones = keep.tile([P, P], BF16, name="ones")
+        nc.vector.memset(ones[:], 1.0)
+
+        words = {}
+
+        def load_weight(w):
+            words[w] = keep.tile([P, 2 * FEAT], U8, name="words_" + w, align_bytes=64)
+            nc.sync.dma_start(
+                out=words[w][:].bitcast(I32),
+                in_=weight_words[w].rearrange("g p b -> (g p) b").bitcast(I32),
+            )
+            scale_rows = weight_scales[w].rearrange("g q n -> (g q) n")
+            for quad in range(4):
+                nc.sync.dma_start(
+                    out=planes[32 * quad : 32 * quad + 4, weight_names.index(w), :].bitcast(I32),
+                    in_=scale_rows[4 * quad : 4 * quad + 4, :].bitcast(I32),
+                )
+
+        def weight_plane(w):
+            return planes[:, weight_names.index(w), :]
+
+        tiles = {}
+
+        def load_activations(u):
+            tiles[u] = {}
+            for name, tensor in (("x", x), ("h", h_prev)):
+                rows = loads.tile([P, ROW_TILES, FEAT], BF16, name=name + "_rows")
+                nc.sync.dma_start(out=rows[:], in_=unit_view(tensor, u))
+                tiles[u][name] = rows
+
+        def load_m_prev(u):
+            rows = loads.tile([P, ROW_TILES, FEAT], BF16, name="m_rows")
+            nc.sync.dma_start(out=rows[:], in_=unit_view(m_prev, u))
+            tiles[u]["m"] = rows
+
+        def transpose_in(u):
+            for name in ("x", "h"):
+                row_words = tiles[u][name][:].rearrange("p j k -> p (j k)").bitcast(F32)
+                grouped = regroup.tile([P, 4 * UNIT_ROWS], BF16, name=name + "_grouped", align_bytes=64)
+                grouped_words = grouped[:].bitcast(F32).rearrange("p (c v) -> p c v", v=2)
+                for pair in range(ROW_TILES // 2):
+                    bank = turn.tile([P, 2, 2, P], F32, name="words_T", tag="turn")
+                    for jj in range(2):
+                        first = (2 * pair + jj) * WORDS
+                        for v in range(2):
+                            nc.tensor.transpose(
+                                out=bank[:, jj, v, :],
+                                in_=row_words[:, first + v : first + WORDS : 2],
+                                identity=ident_f32[:],
+                            )
+                    nc.vector.tensor_copy(
+                        out=grouped_words[:, 2 * pair * P : (2 * pair + 2) * P, :].rearrange(
+                            "p (jj r) v -> p jj r v", jj=2
+                        ),
+                        in_=bank[:].rearrange("p jj v r -> p jj r v"),
+                    )
+                tiles[u][name + "_grouped"] = grouped
+
+        def quantise(u, name):
+            codes = quant.tile([P, UNIT_ROWS], U32, name=name + "_codes", align_bytes=64)
+            scales = quant.tile([P, UNIT_ROWS], U8, name=name + "_scales", align_bytes=64)
+            nc.vector.quantize_mx(
+                out=codes[:].bitcast(FP8X4), scales=scales[:], in_=tiles[u][name + "_grouped"][:]
+            )
+            tiles[u][name + "_codes"] = codes
+            tiles[u][name + "_scales"] = scales
+
+        def forget_gate_exp(u):
+            t = tiles[u]
+            soft = work.tile([P, OUT_CHUNKS, UNIT_ROWS], F32, name="soft_T")
+            for c in range(OUT_CHUNKS):
+                acc = sums.tile([P, UNIT_ROWS], F32, name="f_T", tag="sums")
+                for name, first in (("x", True), ("h", False)):
+                    nc.tensor.matmul_mx(
+                        out=acc[:],
+                        lhsT=words["f_" + name][:, 2 * c * P : 2 * (c + 1) * P].bitcast(FP4X4),
+                        lhsT_scale=weight_plane("f_" + name)[:, c * P : (c + 1) * P],
+                        rhs=t[name + "_codes"][:].bitcast(FP8X4),
+                        rhs_scale=t[name + "_scales"][:],
+                        start=first,
+                        stop=not first,
+                    )
+                nc.scalar.activation(
+                    out=soft[:, c, :], in_=acc[:], func=ACT.Exp, bias=neg_bf[:, c : c + 1], scale=-1.0
+                )
+            t["soft_T"] = soft
+
+        def clamp(u):
+            flat = tiles[u]["soft_T"][:].rearrange("p c r -> p (c r)")
+            nc.vector.tensor_scalar(
+                out=flat, in0=flat, scalar1=1.0, scalar2=1.0e8, op0=ALU.add, op1=ALU.min
+            )
+
+        def log(u):
+            flat = tiles[u]["soft_T"][:].rearrange("p c r -> p (c r)")
+            nc.scalar.activation(out=flat, in_=flat, func=ACT.Ln)
+
+        def transpose_back(u):
+            t = tiles[u]
+            diff = work.tile([P, ROW_TILES, FEAT], F32, name="diff")
+            for j in range(ROW_TILES):
+                bank = turn.tile([P, FEAT], F32, name="soft_rows", tag="turn")
+                for c in range(OUT_CHUNKS):
+                    nc.tensor.transpose(
+                        out=bank[:, c * P : (c + 1) * P],
+                        in_=t["soft_T"][:, c, j * P : (j + 1) * P],
+                        identity=ident_f32[:],
+                    )
+                nc.vector.tensor_tensor(out=diff[:, j, :], in0=bank[:], in1=t["m"][:, j, :], op=ALU.subtract)
+            t["diff"] = diff
+
+        def input_gate(u):
+            t = tiles[u]
+            gate = work.tile([P, ROW_TILES, FEAT], F32, name="gate")
+            for j in range(ROW_TILES):
+                acc = sums.tile([P, FEAT], F32, name="i_rows", tag="sums")
+                for name, first in (("x", True), ("h", False)):
+                    nc.tensor.matmul_mx(
+                        out=acc[:],
+                        lhsT=t[name + "_codes"][:, j * P : (j + 1) * P].bitcast(FP8X4),
+                        lhsT_scale=t[name + "_scales"][:, j * P : (j + 1) * P],
+                        rhs=words["i_" + name][:].bitcast(FP4X4),
+                        rhs_scale=weight_plane("i_" + name),
+                        start=first,
+                        stop=not first,
+                    )
+                nc.vector.tensor_tensor(out=gate[:, j, :], in0=acc[:], in1=bias_i[:], op=ALU.add)
+            t["gate"] = gate
+
+        load_activations(0)
+        load_weight("f_x")
+        load_weight("f_h")
+        nc.sync.dma_start(out=bf_rows[0:OUT_CHUNKS, :], in_=b_f.rearrange("(c n) -> c n", c=OUT_CHUNKS))
+        load_activations(1)
+        load_weight("i_x")
+        load_weight("i_h")
+        nc.sync.dma_start(out=bi_row[0:1, :], in_=b_i.rearrange("(o n) -> o n", o=1))
+        load_activations(2)
+        load_m_prev(0)
+
+        transpose_in(0)
+        quantise(0, "x")
+        quantise(0, "h")
+        transpose_in(1)
+
+        bf_T = turn.tile([P, P], BF16, name="bf_T", tag="turn")
+        nc.tensor.transpose(out=bf_T[:], in_=bf_rows[:], identity=ident_bf16[:])
+        neg_bf = keep.tile([P, OUT_CHUNKS], F32, name="neg_bf")
+        nc.vector.tensor_scalar_mul(out=neg_bf[:], in0=bf_T[:, 0:OUT_CHUNKS], scalar1=-1.0)
+        bi_sum = sums.tile([P, FEAT], F32, name="bi_sum", tag="sums")
+        nc.tensor.matmul(out=bi_sum[:], lhsT=ones[:], rhs=bi_row[:], start=True, stop=True)
+        bias_i = keep.tile([P, FEAT], F32, name="bias_i")
+        nc.vector.tensor_copy(out=bias_i[:], in_=bi_sum[:])
+
+        for s in range(N_UNITS + 1):
+            if s + 3 < N_UNITS:
+                load_activations(s + 3)
+            if s + 1 < N_UNITS:
+                load_m_prev(s + 1)
+            if s < N_UNITS:
+                forget_gate_exp(s)
+            if s >= 1:
+                transpose_back(s - 1)
+            if s < N_UNITS:
+                clamp(s)
+                log(s)
+            if s >= 1:
+                t = tiles[s - 1]
+                diff = t["diff"][:].rearrange("p j n -> p (j n)")
+                gate = t["gate"][:].rearrange("p j n -> p (j n)")
+                nc.vector.tensor_tensor(out=diff, in0=gate, in1=diff, op=ALU.add)
+            if s + 1 < N_UNITS:
+                quantise(s + 1, "x")
+            if s >= 1:
+                below = short.tile([P, ROW_TILES, FEAT], F32, name="below")
+                nc.vector.tensor_scalar_min(out=below[:].rearrange("p j n -> p (j n)"), in0=diff, scalar1=0.0)
+            if s + 1 < N_UNITS:
+                quantise(s + 1, "h")
+            if s >= 1:
+                above = work.tile([P, ROW_TILES, FEAT], F32, name="above")
+                above_flat = above[:].rearrange("p j n -> p (j n)")
+                nc.vector.tensor_scalar_max(out=above_flat, in0=diff, scalar1=0.0)
+                nc.scalar.activation(out=diff, in_=below[:].rearrange("p j n -> p (j n)"), func=ACT.Exp)
+                nc.sync.dma_start(out=unit_view(out_1, s - 1), in_=t["diff"][:])
+                nc.scalar.activation(out=above_flat, in_=above_flat, func=ACT.Exp, scale=-1.0)
+                nc.sync.dma_start(out=unit_view(out_2, s - 1), in_=above[:])
+                for j in range(ROW_TILES):
+                    nc.gpsimd.tensor_tensor(
+                        out=t["gate"][:, j, :], in0=t["gate"][:, j, :], in1=below[:, j, :], op=ALU.subtract
+                    )
+            if s < N_UNITS:
+                input_gate(s)
+            if s + 2 < N_UNITS:
+                transpose_in(s + 2)
+            if s >= 1:
+                nc.sync.dma_start(out=unit_view(out_0, s - 1), in_=t["gate"][:])

@@ -76,6 +76,8 @@ def tile_slstmlayer_pa_t_kernel(
         nc.vector.memset(bi_row[:], 0.0)
         ones = keep.tile([P, P], BF16, name="ones")
         nc.vector.memset(ones[:], 1.0)
+        neg_ident = keep.tile([P, P], BF16, name="neg_ident")
+        nc.vector.tensor_scalar_mul(out=neg_ident[:], in0=ident_bf16[:], scalar1=-1.0)
 
         words = {}
 
@@ -171,18 +173,22 @@ def tile_slstmlayer_pa_t_kernel(
             flat = tiles[u]["soft_T"][:].rearrange("p c r -> p (c r)")
             nc.scalar.activation(out=flat, in_=flat, func=ACT.Ln)
 
-        def transpose_back(u):
+        def difference(u):
             t = tiles[u]
             diff = work.tile([P, ROW_TILES, FEAT], F32, name="diff")
             for j in range(ROW_TILES):
-                bank = turn.tile([P, FEAT], F32, name="soft_rows", tag="turn")
+                bank = turn.tile([P, FEAT], F32, name="s_minus_m", tag="turn")
+                nc.tensor.matmul(out=bank[:], lhsT=neg_ident[:], rhs=t["m"][:, j, :], start=True, stop=False)
                 for c in range(OUT_CHUNKS):
-                    nc.tensor.transpose(
+                    nc.tensor.matmul(
                         out=bank[:, c * P : (c + 1) * P],
-                        in_=t["soft_T"][:, c, j * P : (j + 1) * P],
-                        identity=ident_f32[:],
+                        lhsT=t["soft_T"][:, c, j * P : (j + 1) * P],
+                        rhs=ident_f32[:],
+                        is_transpose=True,
+                        start=False,
+                        stop=(c == OUT_CHUNKS - 1),
                     )
-                nc.vector.tensor_tensor(out=diff[:, j, :], in0=bank[:], in1=t["m"][:, j, :], op=ALU.subtract)
+                nc.vector.tensor_tensor(out=diff[:, j, :], in0=bank[:], in1=t["gate"][:, j, :], op=ALU.add)
             t["diff"] = diff
 
         def input_gate(u):
@@ -236,15 +242,13 @@ def tile_slstmlayer_pa_t_kernel(
             if s < N_UNITS:
                 forget_gate_exp(s)
             if s >= 1:
-                transpose_back(s - 1)
+                difference(s - 1)
             if s < N_UNITS:
                 clamp(s)
                 log(s)
             if s >= 1:
                 t = tiles[s - 1]
                 diff = t["diff"][:].rearrange("p j n -> p (j n)")
-                gate = t["gate"][:].rearrange("p j n -> p (j n)")
-                nc.vector.tensor_tensor(out=diff, in0=gate, in1=diff, op=ALU.add)
             if s + 1 < N_UNITS:
                 quantise(s + 1, "x")
             if s >= 1:

@@ -175,7 +175,7 @@ def tile_slstmlayer_pa_t_kernel(
 
         def difference(u):
             t = tiles[u]
-            diff = work.tile([P, ROW_TILES, FEAT], F32, name="diff")
+            diff = short.tile([P, ROW_TILES, FEAT], F32, name="diff")
             for j in range(ROW_TILES):
                 bank = turn.tile([P, FEAT], F32, name="s_minus_m", tag="turn")
                 nc.tensor.matmul(out=bank[:], lhsT=neg_ident[:], rhs=t["m"][:, j, :], start=True, stop=False)
@@ -210,30 +210,30 @@ def tile_slstmlayer_pa_t_kernel(
             t["gate"] = gate
 
         load_activations(0)
+        nc.sync.dma_start(out=bf_rows[0:OUT_CHUNKS, :], in_=b_f.rearrange("(c n) -> c n", c=OUT_CHUNKS))
+        nc.sync.dma_start(out=bi_row[0:1, :], in_=b_i.rearrange("(o n) -> o n", o=1))
         load_weight("f_x")
         load_weight("f_h")
-        nc.sync.dma_start(out=bf_rows[0:OUT_CHUNKS, :], in_=b_f.rearrange("(c n) -> c n", c=OUT_CHUNKS))
         load_activations(1)
         load_weight("i_x")
         load_weight("i_h")
-        nc.sync.dma_start(out=bi_row[0:1, :], in_=b_i.rearrange("(o n) -> o n", o=1))
         load_activations(2)
         load_m_prev(0)
 
         transpose_in(0)
-        quantise(0, "x")
-        quantise(0, "h")
-        transpose_in(1)
-
         bf_T = turn.tile([P, P], BF16, name="bf_T", tag="turn")
         nc.tensor.transpose(out=bf_T[:], in_=bf_rows[:], identity=ident_bf16[:])
         neg_bf = keep.tile([P, OUT_CHUNKS], F32, name="neg_bf")
         nc.vector.tensor_scalar_mul(out=neg_bf[:], in0=bf_T[:, 0:OUT_CHUNKS], scalar1=-1.0)
+        quantise(0, "x")
+        quantise(0, "h")
+        transpose_in(1)
         bi_sum = sums.tile([P, FEAT], F32, name="bi_sum", tag="sums")
         nc.tensor.matmul(out=bi_sum[:], lhsT=ones[:], rhs=bi_row[:], start=True, stop=True)
         bias_i = keep.tile([P, FEAT], F32, name="bias_i")
         nc.vector.tensor_copy(out=bias_i[:], in_=bi_sum[:])
 
+        halves = (slice(0, ROW_TILES // 2), slice(ROW_TILES // 2, ROW_TILES))
         for s in range(N_UNITS + 1):
             if s + 3 < N_UNITS:
                 load_activations(s + 3)
@@ -258,19 +258,30 @@ def tile_slstmlayer_pa_t_kernel(
                 quantise(s + 1, "h")
             if s >= 1:
                 above = work.tile([P, ROW_TILES, FEAT], F32, name="above")
-                above_flat = above[:].rearrange("p j n -> p (j n)")
-                nc.vector.tensor_scalar_max(out=above_flat, in0=diff, scalar1=0.0)
-                nc.scalar.activation(out=diff, in_=below[:].rearrange("p j n -> p (j n)"), func=ACT.Exp)
-                nc.sync.dma_start(out=unit_view(out_1, s - 1), in_=t["diff"][:])
-                nc.scalar.activation(out=above_flat, in_=above_flat, func=ACT.Exp, scale=-1.0)
-                nc.sync.dma_start(out=unit_view(out_2, s - 1), in_=above[:])
+                nc.vector.tensor_scalar_max(out=above[:].rearrange("p j n -> p (j n)"), in0=diff, scalar1=0.0)
+                subtractor = nc.gpsimd if s < N_UNITS else nc.vector
                 for j in range(ROW_TILES):
-                    nc.gpsimd.tensor_tensor(
+                    subtractor.tensor_tensor(
                         out=t["gate"][:, j, :], in0=t["gate"][:, j, :], in1=below[:, j, :], op=ALU.subtract
                     )
+                i_out = work.tile([P, ROW_TILES, FEAT], F32, name="i_out")
+                for half in halves:
+                    nc.scalar.activation(
+                        out=i_out[:, half, :].rearrange("p j n -> p (j n)"),
+                        in_=below[:, half, :].rearrange("p j n -> p (j n)"),
+                        func=ACT.Exp,
+                    )
+                    nc.sync.dma_start(out=unit_view(out_1, s - 1)[:, half, :], in_=i_out[:, half, :])
+                for half in halves:
+                    nc.sync.dma_start(out=unit_view(out_0, s - 1)[:, half, :], in_=t["gate"][:, half, :])
+                    nc.scalar.activation(
+                        out=above[:, half, :].rearrange("p j n -> p (j n)"),
+                        in_=above[:, half, :].rearrange("p j n -> p (j n)"),
+                        func=ACT.Exp,
+                        scale=-1.0,
+                    )
+                    nc.sync.dma_start(out=unit_view(out_2, s - 1)[:, half, :], in_=above[:, half, :])
             if s < N_UNITS:
                 input_gate(s)
             if s + 2 < N_UNITS:
                 transpose_in(s + 2)
-            if s >= 1:
-                nc.sync.dma_start(out=unit_view(out_0, s - 1), in_=t["gate"][:])

@@ -54,7 +54,7 @@ def tile_slstmlayer_pa_t_kernel(
         short = stack.enter_context(tc.tile_pool(name="short", bufs=2))
         turn = stack.enter_context(tc.psum_pool(name="turn", bufs=4))
         sums = stack.enter_context(tc.psum_pool(name="sums", bufs=4))
-        stack.enter_context(tc.manual_schedule())
+        stack.enter_context(tc.manual_schedule(engines={mybir.EngineType.Activation}))
 
         def unit_view(tensor, u):
             rows = tensor[u * UNIT_ROWS : (u + 1) * UNIT_ROWS, :]

@@ -21,6 +21,15 @@ UNIT_ROWS = P * ROW_TILES
 N_UNITS = BATCH // UNIT_ROWS
 OUT_CHUNKS = FEAT // P
 WORDS = FEAT // 2
+RUN = 2
+SCALAR_DRAINS = ()
+HEAD_UNITS = 0
+HEAD_DRAINS = (1, 3)
+
+SOFT_BUFS = 4
+GATE_BUFS = 3
+VBANKS = 4
+QUANT_BUFS = 6
 
 FLOPS = 2 * BATCH * FEAT * FEAT * 4
 
@@ -47,13 +56,15 @@ def tile_slstmlayer_pa_t_kernel(
     nc = tc.nc
     with ExitStack() as stack:
         keep = stack.enter_context(tc.tile_pool(name="keep", bufs=1))
-        loads = stack.enter_context(tc.tile_pool(name="loads", bufs=3))
+        loads = stack.enter_context(tc.tile_pool(name="loads", bufs=4))
         regroup = stack.enter_context(tc.tile_pool(name="regroup", bufs=2))
-        quant = stack.enter_context(tc.tile_pool(name="quant", bufs=3))
-        work = stack.enter_context(tc.tile_pool(name="work", bufs=3))
-        short = stack.enter_context(tc.tile_pool(name="short", bufs=2))
-        turn = stack.enter_context(tc.psum_pool(name="turn", bufs=4))
-        sums = stack.enter_context(tc.psum_pool(name="sums", bufs=4))
+        quant = stack.enter_context(tc.tile_pool(name="quant", bufs=QUANT_BUFS))
+        soft_pool = stack.enter_context(tc.tile_pool(name="soft_pool", bufs=SOFT_BUFS))
+        gate_pool = stack.enter_context(tc.tile_pool(name="gate_pool", bufs=GATE_BUFS))
+        outs = stack.enter_context(tc.tile_pool(name="outs", bufs=2))
+        short = stack.enter_context(tc.tile_pool(name="short", bufs=3))
+        vbanks = stack.enter_context(tc.psum_pool(name="vbanks", bufs=VBANKS))
+        sbanks = stack.enter_context(tc.psum_pool(name="sbanks", bufs=4))
         stack.enter_context(tc.manual_schedule(engines={mybir.EngineType.Activation}))
 
         def unit_view(tensor, u):
@@ -98,6 +109,11 @@ def tile_slstmlayer_pa_t_kernel(
             return planes[:, weight_names.index(w), :]
 
         tiles = {}
+        halves = (slice(0, ROW_TILES // 2), slice(ROW_TILES // 2, ROW_TILES))
+        whole = slice(0, ROW_TILES)
+
+        def flat(view):
+            return view.rearrange("p j n -> p (j n)")
 
         def load_activations(u):
             tiles[u] = {}
@@ -112,12 +128,14 @@ def tile_slstmlayer_pa_t_kernel(
             tiles[u]["m"] = rows
 
         def transpose_in(u):
-            for name in ("x", "h"):
+            scalar_share = HEAD_DRAINS if u < HEAD_UNITS else SCALAR_DRAINS
+            for n, name in enumerate(("x", "h")):
                 row_words = tiles[u][name][:].rearrange("p j k -> p (j k)").bitcast(F32)
                 grouped = regroup.tile([P, 4 * UNIT_ROWS], BF16, name=name + "_grouped", align_bytes=64)
                 grouped_words = grouped[:].bitcast(F32).rearrange("p (c v) -> p c v", v=2)
                 for pair in range(ROW_TILES // 2):
-                    bank = turn.tile([P, 2, 2, P], F32, name="words_T", tag="turn")
+                    by_scalar = (2 * n + pair) in scalar_share
+                    bank = vbanks.tile([P, 2, 2, P], F32, name="words_T", tag="vbank")
                     for jj in range(2):
                         first = (2 * pair + jj) * WORDS
                         for v in range(2):
@@ -126,12 +144,13 @@ def tile_slstmlayer_pa_t_kernel(
                                 in_=row_words[:, first + v : first + WORDS : 2],
                                 identity=ident_f32[:],
                             )
-                    nc.vector.tensor_copy(
-                        out=grouped_words[:, 2 * pair * P : (2 * pair + 2) * P, :].rearrange(
-                            "p (jj r) v -> p jj r v", jj=2
-                        ),
-                        in_=bank[:].rearrange("p jj v r -> p jj r v"),
+                    target = grouped_words[:, 2 * pair * P : (2 * pair + 2) * P, :].rearrange(
+                        "p (jj r) v -> p jj r v", jj=2
                     )
+                    if by_scalar:
+                        nc.scalar.copy(out=target, in_=bank[:].rearrange("p jj v r -> p jj r v"))
+                    else:
+                        nc.vector.tensor_copy(out=target, in_=bank[:].rearrange("p jj v r -> p jj r v"))
                 tiles[u][name + "_grouped"] = grouped
 
         def quantise(u, name):
@@ -143,11 +162,11 @@ def tile_slstmlayer_pa_t_kernel(
             tiles[u][name + "_codes"] = codes
             tiles[u][name + "_scales"] = scales
 
-        def forget_gate_exp(u):
+        def forget_gate(u):
             t = tiles[u]
-            soft = work.tile([P, OUT_CHUNKS, UNIT_ROWS], F32, name="soft_T")
+            t["f_T"] = []
             for c in range(OUT_CHUNKS):
-                acc = sums.tile([P, UNIT_ROWS], F32, name="f_T", tag="sums")
+                acc = sbanks.tile([P, UNIT_ROWS], F32, name="f_T", tag="sbank")
                 for name, first in (("x", True), ("h", False)):
                     nc.tensor.matmul_mx(
                         out=acc[:],
@@ -158,44 +177,32 @@ def tile_slstmlayer_pa_t_kernel(
                         start=first,
                         stop=not first,
                     )
+                t["f_T"].append(acc)
+
+        def forget_exp(u):
+            t = tiles[u]
+            soft = soft_pool.tile([P, OUT_CHUNKS, UNIT_ROWS], F32, name="soft_T")
+            for c in range(OUT_CHUNKS):
                 nc.scalar.activation(
-                    out=soft[:, c, :], in_=acc[:], func=ACT.Exp, bias=neg_bf[:, c : c + 1], scale=-1.0
+                    out=soft[:, c, :], in_=t["f_T"][c][:], func=ACT.Exp, bias=neg_bf[:, c : c + 1], scale=-1.0
                 )
             t["soft_T"] = soft
 
         def clamp(u):
-            flat = tiles[u]["soft_T"][:].rearrange("p c r -> p (c r)")
-            nc.vector.tensor_scalar(
-                out=flat, in0=flat, scalar1=1.0, scalar2=1.0e8, op0=ALU.add, op1=ALU.min
-            )
+            whole = tiles[u]["soft_T"][:].rearrange("p c r -> p (c r)")
+            nc.vector.tensor_scalar_min(out=whole, in0=whole, scalar1=1.0e8 - 1.0)
 
         def log(u):
-            flat = tiles[u]["soft_T"][:].rearrange("p c r -> p (c r)")
-            nc.scalar.activation(out=flat, in_=flat, func=ACT.Ln)
-
-        def difference(u):
-            t = tiles[u]
-            diff = short.tile([P, ROW_TILES, FEAT], F32, name="diff")
-            for j in range(ROW_TILES):
-                bank = turn.tile([P, FEAT], F32, name="s_minus_m", tag="turn")
-                nc.tensor.matmul(out=bank[:], lhsT=neg_ident[:], rhs=t["m"][:, j, :], start=True, stop=False)
-                for c in range(OUT_CHUNKS):
-                    nc.tensor.matmul(
-                        out=bank[:, c * P : (c + 1) * P],
-                        lhsT=t["soft_T"][:, c, j * P : (j + 1) * P],
-                        rhs=ident_f32[:],
-                        is_transpose=True,
-                        start=False,
-                        stop=(c == OUT_CHUNKS - 1),
-                    )
-                nc.vector.tensor_tensor(out=diff[:, j, :], in0=bank[:], in1=t["gate"][:, j, :], op=ALU.add)
-            t["diff"] = diff
+            soft = tiles[u]["soft_T"]
+            for r in range(2):
+                part = soft[:, :, r * UNIT_ROWS // 2 : (r + 1) * UNIT_ROWS // 2]
+                nc.scalar.activation(out=part, in_=part, func=ACT.Ln, bias=1.0)
 
         def input_gate(u):
             t = tiles[u]
-            gate = work.tile([P, ROW_TILES, FEAT], F32, name="gate")
+            gate = gate_pool.tile([P, ROW_TILES, FEAT], F32, name="gate")
             for j in range(ROW_TILES):
-                acc = sums.tile([P, FEAT], F32, name="i_rows", tag="sums")
+                acc = vbanks.tile([P, FEAT], F32, name="i_rows", tag="vbank")
                 for name, first in (("x", True), ("h", False)):
                     nc.tensor.matmul_mx(
                         out=acc[:],
@@ -209,79 +216,117 @@ def tile_slstmlayer_pa_t_kernel(
                 nc.vector.tensor_tensor(out=gate[:, j, :], in0=acc[:], in1=bias_i[:], op=ALU.add)
             t["gate"] = gate
 
+        def difference(u, row_tiles):
+            t = tiles[u]
+            if "diff" not in t:
+                t["diff"] = short.tile([P, ROW_TILES, FEAT], F32, name="diff")
+                t["below"] = short.tile([P, ROW_TILES, FEAT], F32, name="below")
+            for j in row_tiles:
+                bank = vbanks.tile([P, FEAT], F32, name="s_minus_m", tag="vbank")
+                nc.tensor.matmul(out=bank[:], lhsT=neg_ident[:], rhs=t["m"][:, j, :], start=True, stop=False)
+                for c in range(OUT_CHUNKS):
+                    nc.tensor.matmul(
+                        out=bank[:, c * P : (c + 1) * P],
+                        lhsT=t["soft_T"][:, c, j * P : (j + 1) * P],
+                        rhs=ident_f32[:],
+                        is_transpose=True,
+                        start=False,
+                        stop=(c == OUT_CHUNKS - 1),
+                    )
+                nc.vector.tensor_tensor(out=t["diff"][:, j, :], in0=bank[:], in1=t["gate"][:, j, :], op=ALU.add)
+
+        def negative_part(u, part):
+            t = tiles[u]
+            nc.vector.tensor_scalar_min(out=flat(t["below"][:, part, :]), in0=flat(t["diff"][:, part, :]), scalar1=0.0)
+
+        def positive_part(u, part):
+            t = tiles[u]
+            nc.vector.tensor_scalar_max(out=flat(t["diff"][:, part, :]), in0=flat(t["diff"][:, part, :]), scalar1=0.0)
+
+        def new_maximum(u, part, engine):
+            t = tiles[u]
+            for j in range(part.start, part.stop):
+                engine.tensor_tensor(out=t["gate"][:, j, :], in0=t["gate"][:, j, :], in1=t["below"][:, j, :], op=ALU.subtract)
+                if j % 2 == 1:
+                    half = halves[j // 2]
+                    nc.sync.dma_start(out=unit_view(out_0, u)[:, half, :], in_=t["gate"][:, half, :])
+
+        def final_exp(u):
+            t = tiles[u]
+            i_out = outs.tile([P, ROW_TILES, FEAT], F32, name="i_out")
+            for half in halves:
+                nc.scalar.activation(out=flat(t["diff"][:, half, :]), in_=flat(t["diff"][:, half, :]), func=ACT.Exp, scale=-1.0)
+                nc.sync.dma_start(out=unit_view(out_2, u)[:, half, :], in_=t["diff"][:, half, :])
+                nc.scalar.activation(out=flat(i_out[:, half, :]), in_=flat(t["below"][:, half, :]), func=ACT.Exp)
+                nc.sync.dma_start(out=unit_view(out_1, u)[:, half, :], in_=i_out[:, half, :])
+
+
         load_activations(0)
+        load_activations(1)
         nc.sync.dma_start(out=bf_rows[0:OUT_CHUNKS, :], in_=b_f.rearrange("(c n) -> c n", c=OUT_CHUNKS))
-        nc.sync.dma_start(out=bi_row[0:1, :], in_=b_i.rearrange("(o n) -> o n", o=1))
         load_weight("f_x")
         load_weight("f_h")
-        load_activations(1)
+        load_activations(2)
+        nc.sync.dma_start(out=bi_row[0:1, :], in_=b_i.rearrange("(o n) -> o n", o=1))
         load_weight("i_x")
         load_weight("i_h")
-        load_activations(2)
+        load_activations(3)
         load_m_prev(0)
+        load_m_prev(1)
 
         transpose_in(0)
-        bf_T = turn.tile([P, P], BF16, name="bf_T", tag="turn")
+        bf_T = sbanks.tile([P, P], BF16, name="bf_T", tag="sbank")
         nc.tensor.transpose(out=bf_T[:], in_=bf_rows[:], identity=ident_bf16[:])
         neg_bf = keep.tile([P, OUT_CHUNKS], F32, name="neg_bf")
+        bias_i = keep.tile([P, FEAT], F32, name="bias_i")
+
         nc.vector.tensor_scalar_mul(out=neg_bf[:], in0=bf_T[:, 0:OUT_CHUNKS], scalar1=-1.0)
         quantise(0, "x")
         quantise(0, "h")
+        forget_gate(0)
         transpose_in(1)
-        bi_sum = sums.tile([P, FEAT], F32, name="bi_sum", tag="sums")
-        nc.tensor.matmul(out=bi_sum[:], lhsT=ones[:], rhs=bi_row[:], start=True, stop=True)
-        bias_i = keep.tile([P, FEAT], F32, name="bias_i")
-        nc.vector.tensor_copy(out=bias_i[:], in_=bi_sum[:])
-
-        halves = (slice(0, ROW_TILES // 2), slice(ROW_TILES // 2, ROW_TILES))
-        for s in range(N_UNITS + 1):
-            if s + 3 < N_UNITS:
-                load_activations(s + 3)
-            if s + 1 < N_UNITS:
+        quantise(1, "x")
+        quantise(1, "h")
+        for s in range(N_UNITS + 3):
+            middle = s - 2
+            last = s - 3
+            if s + 4 < N_UNITS:
+                load_activations(s + 4)
+            if 2 <= s + 1 < N_UNITS:
                 load_m_prev(s + 1)
             if s < N_UNITS:
-                forget_gate_exp(s)
-            if s >= 1:
-                difference(s - 1)
-            if s < N_UNITS:
-                clamp(s)
-                log(s)
-            if s >= 1:
-                t = tiles[s - 1]
-                diff = t["diff"][:].rearrange("p j n -> p (j n)")
-            if s + 1 < N_UNITS:
-                quantise(s + 1, "x")
-            if s >= 1:
-                below = short.tile([P, ROW_TILES, FEAT], F32, name="below")
-                nc.vector.tensor_scalar_min(out=below[:].rearrange("p j n -> p (j n)"), in0=diff, scalar1=0.0)
-            if s + 1 < N_UNITS:
-                quantise(s + 1, "h")
-            if s >= 1:
-                above = work.tile([P, ROW_TILES, FEAT], F32, name="above")
-                nc.vector.tensor_scalar_max(out=above[:].rearrange("p j n -> p (j n)"), in0=diff, scalar1=0.0)
-                subtractor = nc.gpsimd if s < N_UNITS else nc.vector
-                for j in range(ROW_TILES):
-                    subtractor.tensor_tensor(
-                        out=t["gate"][:, j, :], in0=t["gate"][:, j, :], in1=below[:, j, :], op=ALU.subtract
-                    )
-                i_out = work.tile([P, ROW_TILES, FEAT], F32, name="i_out")
-                for half in halves:
-                    nc.scalar.activation(
-                        out=i_out[:, half, :].rearrange("p j n -> p (j n)"),
-                        in_=below[:, half, :].rearrange("p j n -> p (j n)"),
-                        func=ACT.Exp,
-                    )
-                    nc.sync.dma_start(out=unit_view(out_1, s - 1)[:, half, :], in_=i_out[:, half, :])
-                for half in halves:
-                    nc.sync.dma_start(out=unit_view(out_0, s - 1)[:, half, :], in_=t["gate"][:, half, :])
-                    nc.scalar.activation(
-                        out=above[:, half, :].rearrange("p j n -> p (j n)"),
-                        in_=above[:, half, :].rearrange("p j n -> p (j n)"),
-                        func=ACT.Exp,
-                        scale=-1.0,
-                    )
-                    nc.sync.dma_start(out=unit_view(out_2, s - 1)[:, half, :], in_=above[:, half, :])
-            if s < N_UNITS:
-                input_gate(s)
+                forget_exp(s)
+            if middle == 0:
+                bi_sum = vbanks.tile([P, FEAT], F32, name="bi_sum", tag="vbank")
+                nc.tensor.matmul(out=bi_sum[:], lhsT=ones[:], rhs=bi_row[:], start=True, stop=True)
+                nc.vector.tensor_copy(out=bias_i[:], in_=bi_sum[:])
+            if 0 <= middle < N_UNITS:
+                input_gate(middle)
             if s + 2 < N_UNITS:
                 transpose_in(s + 2)
+            if 0 <= last < N_UNITS:
+                final_exp(last)
+            if middle == N_UNITS - 1:
+                for half in halves:
+                    difference(middle, range(half.start, half.stop))
+                    negative_part(middle, half)
+                    positive_part(middle, half)
+                    new_maximum(middle, half, nc.vector)
+            elif 0 <= middle < N_UNITS:
+                difference(middle, range(ROW_TILES))
+            if s < N_UNITS:
+                clamp(s)
+            if s + 2 < N_UNITS:
+                quantise(s + 2, "x")
+            if 0 <= middle < N_UNITS - 1:
+                negative_part(middle, whole)
+            if s + 2 < N_UNITS:
+                quantise(s + 2, "h")
+            if 0 <= middle < N_UNITS - 1:
+                positive_part(middle, whole)
+                new_maximum(middle, whole, nc.gpsimd)
+            if s + 1 < N_UNITS:
+                forget_gate(s + 1)
+            if s < N_UNITS and s % RUN == RUN - 1:
+                for u in range(s - RUN + 1, s + 1):
+                    log(u)

@@ -65,7 +65,7 @@ def tile_slstmlayer_pa_t_kernel(
         short = stack.enter_context(tc.tile_pool(name="short", bufs=3))
         vbanks = stack.enter_context(tc.psum_pool(name="vbanks", bufs=VBANKS))
         sbanks = stack.enter_context(tc.psum_pool(name="sbanks", bufs=4))
-        stack.enter_context(tc.manual_schedule(engines={mybir.EngineType.Activation}))
+        stack.enter_context(tc.manual_schedule())
 
         def unit_view(tensor, u):
             rows = tensor[u * UNIT_ROWS : (u + 1) * UNIT_ROWS, :]
@@ -283,8 +283,8 @@ def tile_slstmlayer_pa_t_kernel(
         nc.vector.tensor_scalar_mul(out=neg_bf[:], in0=bf_T[:, 0:OUT_CHUNKS], scalar1=-1.0)
         quantise(0, "x")
         quantise(0, "h")
-        forget_gate(0)
         transpose_in(1)
+        forget_gate(0)
         quantise(1, "x")
         quantise(1, "h")
         for s in range(N_UNITS + 3):

@@ -300,10 +300,10 @@ def tile_slstmlayer_pa_t_kernel(
                 bi_sum = vbanks.tile([P, FEAT], F32, name="bi_sum", tag="vbank")
                 nc.tensor.matmul(out=bi_sum[:], lhsT=ones[:], rhs=bi_row[:], start=True, stop=True)
                 nc.vector.tensor_copy(out=bias_i[:], in_=bi_sum[:])
-            if 0 <= middle < N_UNITS:
-                input_gate(middle)
             if s + 2 < N_UNITS:
                 transpose_in(s + 2)
+            if 0 <= middle < N_UNITS:
+                input_gate(middle)
             if 0 <= last < N_UNITS:
                 final_exp(last)
             if middle == N_UNITS - 1:

@@ -21,13 +21,14 @@ UNIT_ROWS = P * ROW_TILES
 N_UNITS = BATCH // UNIT_ROWS
 OUT_CHUNKS = FEAT // P
 WORDS = FEAT // 2
-RUN = 2
-SCALAR_DRAINS = ()
-HEAD_UNITS = 0
-HEAD_DRAINS = (1, 3)
+RUN_ENDS = (1, 3, 5, 7)
+BIG = 3.0e38
+LAG = 2
+LOADED = 4
 
 SOFT_BUFS = 4
 GATE_BUFS = 3
+SHORT_BUFS = 3
 VBANKS = 4
 QUANT_BUFS = 6
 
@@ -56,13 +57,12 @@ def tile_slstmlayer_pa_t_kernel(
     nc = tc.nc
     with ExitStack() as stack:
         keep = stack.enter_context(tc.tile_pool(name="keep", bufs=1))
-        loads = stack.enter_context(tc.tile_pool(name="loads", bufs=4))
+        loads = stack.enter_context(tc.tile_pool(name="loads", bufs=LOADED))
         regroup = stack.enter_context(tc.tile_pool(name="regroup", bufs=2))
         quant = stack.enter_context(tc.tile_pool(name="quant", bufs=QUANT_BUFS))
         soft_pool = stack.enter_context(tc.tile_pool(name="soft_pool", bufs=SOFT_BUFS))
         gate_pool = stack.enter_context(tc.tile_pool(name="gate_pool", bufs=GATE_BUFS))
-        outs = stack.enter_context(tc.tile_pool(name="outs", bufs=2))
-        short = stack.enter_context(tc.tile_pool(name="short", bufs=3))
+        short = stack.enter_context(tc.tile_pool(name="short", bufs=SHORT_BUFS))
         vbanks = stack.enter_context(tc.psum_pool(name="vbanks", bufs=VBANKS))
         sbanks = stack.enter_context(tc.psum_pool(name="sbanks", bufs=4))
         stack.enter_context(tc.manual_schedule())
@@ -128,13 +128,11 @@ def tile_slstmlayer_pa_t_kernel(
             tiles[u]["m"] = rows
 
         def transpose_in(u):
-            scalar_share = HEAD_DRAINS if u < HEAD_UNITS else SCALAR_DRAINS
             for n, name in enumerate(("x", "h")):
                 row_words = tiles[u][name][:].rearrange("p j k -> p (j k)").bitcast(F32)
                 grouped = regroup.tile([P, 4 * UNIT_ROWS], BF16, name=name + "_grouped", align_bytes=64)
                 grouped_words = grouped[:].bitcast(F32).rearrange("p (c v) -> p c v", v=2)
                 for pair in range(ROW_TILES // 2):
-                    by_scalar = (2 * n + pair) in scalar_share
                     bank = vbanks.tile([P, 2, 2, P], F32, name="words_T", tag="vbank")
                     for jj in range(2):
                         first = (2 * pair + jj) * WORDS
@@ -147,10 +145,7 @@ def tile_slstmlayer_pa_t_kernel(
                     target = grouped_words[:, 2 * pair * P : (2 * pair + 2) * P, :].rearrange(
                         "p (jj r) v -> p jj r v", jj=2
                     )
-                    if by_scalar:
-                        nc.scalar.copy(out=target, in_=bank[:].rearrange("p jj v r -> p jj r v"))
-                    else:
-                        nc.vector.tensor_copy(out=target, in_=bank[:].rearrange("p jj v r -> p jj r v"))
+                    nc.vector.tensor_copy(out=target, in_=bank[:].rearrange("p jj v r -> p jj r v"))
                 tiles[u][name + "_grouped"] = grouped
 
         def quantise(u, name):
@@ -189,8 +184,9 @@ def tile_slstmlayer_pa_t_kernel(
             t["soft_T"] = soft
 
         def clamp(u):
-            whole = tiles[u]["soft_T"][:].rearrange("p c r -> p (c r)")
-            nc.vector.tensor_scalar_min(out=whole, in0=whole, scalar1=1.0e8 - 1.0)
+            for c in range(0, OUT_CHUNKS, 2):
+                part = flat(tiles[u]["soft_T"][:, c : c + 2, :])
+                nc.gpsimd.tensor_scalar(out=part, in0=part, scalar1=1.0e8 - 1.0, scalar2=0.0, op0=ALU.min, op1=ALU.max)
 
         def log(u):
             soft = tiles[u]["soft_T"]
@@ -233,33 +229,27 @@ def tile_slstmlayer_pa_t_kernel(
                         start=False,
                         stop=(c == OUT_CHUNKS - 1),
                     )
-                nc.vector.tensor_tensor(out=t["diff"][:, j, :], in0=bank[:], in1=t["gate"][:, j, :], op=ALU.add)
-
-        def negative_part(u, part):
-            t = tiles[u]
-            nc.vector.tensor_scalar_min(out=flat(t["below"][:, part, :]), in0=flat(t["diff"][:, part, :]), scalar1=0.0)
-
-        def positive_part(u, part):
-            t = tiles[u]
-            nc.vector.tensor_scalar_max(out=flat(t["diff"][:, part, :]), in0=flat(t["diff"][:, part, :]), scalar1=0.0)
-
-        def new_maximum(u, part, engine):
-            t = tiles[u]
-            for j in range(part.start, part.stop):
-                engine.tensor_tensor(out=t["gate"][:, j, :], in0=t["gate"][:, j, :], in1=t["below"][:, j, :], op=ALU.subtract)
+                i_rows = t["gate"][:, j, :]
+                nc.vector.tensor_tensor(out=t["diff"][:, j, :], in0=bank[:], in1=i_rows, op=ALU.add)
+                nc.vector.scalar_tensor_tensor(
+                    out=i_rows, in0=bank[:], scalar=-1.0, in1=i_rows, op0=ALU.mult, op1=ALU.max
+                )
                 if j % 2 == 1:
                     half = halves[j // 2]
                     nc.sync.dma_start(out=unit_view(out_0, u)[:, half, :], in_=t["gate"][:, half, :])
 
-        def final_exp(u):
-            t = tiles[u]
-            i_out = outs.tile([P, ROW_TILES, FEAT], F32, name="i_out")
-            for half in halves:
-                nc.scalar.activation(out=flat(t["diff"][:, half, :]), in_=flat(t["diff"][:, half, :]), func=ACT.Exp, scale=-1.0)
-                nc.sync.dma_start(out=unit_view(out_2, u)[:, half, :], in_=t["diff"][:, half, :])
-                nc.scalar.activation(out=flat(i_out[:, half, :]), in_=flat(t["below"][:, half, :]), func=ACT.Exp)
-                nc.sync.dma_start(out=unit_view(out_1, u)[:, half, :], in_=i_out[:, half, :])
+        def split_difference(u, half):
+            d = flat(tiles[u]["diff"][:, half, :])
+            below = flat(tiles[u]["below"][:, half, :])
+            nc.gpsimd.tensor_scalar(out=below, in0=d, scalar1=0.0, scalar2=-BIG, op0=ALU.min, op1=ALU.max)
+            nc.gpsimd.tensor_scalar(out=d, in0=d, scalar1=BIG, scalar2=0.0, op0=ALU.min, op1=ALU.max)
 
+        def final_exp(u, half):
+            t = tiles[u]
+            for name, scale, tensor in (("below", 1.0, out_1), ("diff", -1.0, out_2)):
+                part = t[name][:, half, :]
+                nc.scalar.activation(out=flat(part), in_=flat(part), func=ACT.Exp, scale=scale)
+                nc.sync.dma_start(out=unit_view(tensor, u)[:, half, :], in_=part)
 
         load_activations(0)
         load_activations(1)
@@ -287,15 +277,22 @@ def tile_slstmlayer_pa_t_kernel(
         forget_gate(0)
         quantise(1, "x")
         quantise(1, "h")
-        for s in range(N_UNITS + 3):
-            middle = s - 2
-            last = s - 3
-            if s + 4 < N_UNITS:
-                load_activations(s + 4)
-            if 2 <= s + 1 < N_UNITS:
-                load_m_prev(s + 1)
+        ln_done = 0
+        for s in range(N_UNITS + LAG + 1):
+            middle = s - LAG
+            last = middle - 1
+            if s + LOADED < N_UNITS:
+                load_activations(s + LOADED)
+            if 2 <= middle + 3 < N_UNITS:
+                load_m_prev(middle + 3)
             if s < N_UNITS:
                 forget_exp(s)
+            if 0 <= last < N_UNITS:
+                for half in halves:
+                    split_difference(last, half)
+                    final_exp(last, half)
+            if s < N_UNITS:
+                clamp(s)
             if middle == 0:
                 bi_sum = vbanks.tile([P, FEAT], F32, name="bi_sum", tag="vbank")
                 nc.tensor.matmul(out=bi_sum[:], lhsT=ones[:], rhs=bi_row[:], start=True, stop=True)
@@ -304,29 +301,13 @@ def tile_slstmlayer_pa_t_kernel(
                 transpose_in(s + 2)
             if 0 <= middle < N_UNITS:
                 input_gate(middle)
-            if 0 <= last < N_UNITS:
-                final_exp(last)
-            if middle == N_UNITS - 1:
-                for half in halves:
-                    difference(middle, range(half.start, half.stop))
-                    negative_part(middle, half)
-                    positive_part(middle, half)
-                    new_maximum(middle, half, nc.vector)
-            elif 0 <= middle < N_UNITS:
                 difference(middle, range(ROW_TILES))
-            if s < N_UNITS:
-                clamp(s)
             if s + 2 < N_UNITS:
                 quantise(s + 2, "x")
-            if 0 <= middle < N_UNITS - 1:
-                negative_part(middle, whole)
-            if s + 2 < N_UNITS:
                 quantise(s + 2, "h")
-            if 0 <= middle < N_UNITS - 1:
-                positive_part(middle, whole)
-                new_maximum(middle, whole, nc.gpsimd)
             if s + 1 < N_UNITS:
                 forget_gate(s + 1)
-            if s < N_UNITS and s % RUN == RUN - 1:
-                for u in range(s - RUN + 1, s + 1):
+            if s in RUN_ENDS:
+                for u in range(ln_done, s + 1):
                     log(u)
+                ln_done = s + 1

@@ -217,9 +217,12 @@ def tile_slstmlayer_pa_t_kernel(
             if "diff" not in t:
                 t["diff"] = short.tile([P, ROW_TILES, FEAT], F32, name="diff")
                 t["below"] = short.tile([P, ROW_TILES, FEAT], F32, name="below")
+            banks = []
             for j in row_tiles:
                 bank = vbanks.tile([P, FEAT], F32, name="s_minus_m", tag="vbank")
                 nc.tensor.matmul(out=bank[:], lhsT=neg_ident[:], rhs=t["m"][:, j, :], start=True, stop=False)
+                banks.append(bank)
+            for j, bank in zip(row_tiles, banks):
                 for c in range(OUT_CHUNKS):
                     nc.tensor.matmul(
                         out=bank[:, c * P : (c + 1) * P],
@@ -301,7 +304,8 @@ def tile_slstmlayer_pa_t_kernel(
                 transpose_in(s + 2)
             if 0 <= middle < N_UNITS:
                 input_gate(middle)
-                difference(middle, range(ROW_TILES))
+                for half in halves:
+                    difference(middle, range(half.start, half.stop))
             if s + 2 < N_UNITS:
                 quantise(s + 2, "x")
                 quantise(s + 2, "h")

@@ -23,7 +23,15 @@ OUT_CHUNKS = FEAT // P
 WORDS = FEAT // 2
 RUN_ENDS = (1, 3, 5, 7)
 BIG = 3.0e38
-LAG = 2
+SAME = False
+ORDER = {0: "FAQ", 1: "IADQF", 2: "IDFAQ", 3: "IADQF", 4: "IDFAQ", 5: "IADQF", 6: "IDFAQ", 7: "IADQF"}
+LN_FIRST = ()
+EARLY_I = {7: (6, 7)}
+POST = (1, 3, 5)
+M_AHEAD = 3
+LATE = 6
+HEAD = 0
+WARM = 0
 LOADED = 4
 
 SOFT_BUFS = 4
@@ -64,7 +72,7 @@ def tile_slstmlayer_pa_t_kernel(
         gate_pool = stack.enter_context(tc.tile_pool(name="gate_pool", bufs=GATE_BUFS))
         short = stack.enter_context(tc.tile_pool(name="short", bufs=SHORT_BUFS))
         vbanks = stack.enter_context(tc.psum_pool(name="vbanks", bufs=VBANKS))
-        sbanks = stack.enter_context(tc.psum_pool(name="sbanks", bufs=4))
+        sbanks = stack.enter_context(tc.psum_pool(name="sbanks", bufs=8 - VBANKS))
         stack.enter_context(tc.manual_schedule())
 
         def unit_view(tensor, u):
@@ -83,6 +91,9 @@ def tile_slstmlayer_pa_t_kernel(
         nc.vector.memset(planes[:].rearrange("p w n -> p (w n)").bitcast(I32), 0)
         bf_rows = keep.tile([P, P], BF16, name="bf_rows")
         nc.vector.memset(bf_rows[:], 0.0)
+        warm = keep.tile([P, 1], F32, name="warm")
+        nc.vector.memset(warm[:], 0.0)
+        nc.scalar.activation(out=warm[:], in_=warm[:], func=ACT.Exp)
         bi_row = keep.tile([P, FEAT], BF16, name="bi_row")
         nc.vector.memset(bi_row[:], 0.0)
         ones = keep.tile([P, P], BF16, name="ones")
@@ -247,33 +258,39 @@ def tile_slstmlayer_pa_t_kernel(
             nc.gpsimd.tensor_scalar(out=below, in0=d, scalar1=0.0, scalar2=-BIG, op0=ALU.min, op1=ALU.max)
             nc.gpsimd.tensor_scalar(out=d, in0=d, scalar1=BIG, scalar2=0.0, op0=ALU.min, op1=ALU.max)
 
-        def final_exp(u, half):
+        def final_exp(u, half, late_stores=None):
             t = tiles[u]
             for name, scale, tensor in (("below", 1.0, out_1), ("diff", -1.0, out_2)):
                 part = t[name][:, half, :]
                 nc.scalar.activation(out=flat(part), in_=flat(part), func=ACT.Exp, scale=scale)
-                nc.sync.dma_start(out=unit_view(tensor, u)[:, half, :], in_=part)
+                if late_stores is None:
+                    nc.sync.dma_start(out=unit_view(tensor, u)[:, half, :], in_=part)
+                else:
+                    late_stores.append((unit_view(tensor, u)[:, half, :], part))
 
         load_activations(0)
-        load_activations(1)
         nc.sync.dma_start(out=bf_rows[0:OUT_CHUNKS, :], in_=b_f.rearrange("(c n) -> c n", c=OUT_CHUNKS))
+        if HEAD == 0:
+            load_activations(1)
         load_weight("f_x")
         load_weight("f_h")
+        if HEAD == 1:
+            load_activations(1)
         load_activations(2)
         nc.sync.dma_start(out=bi_row[0:1, :], in_=b_i.rearrange("(o n) -> o n", o=1))
         load_weight("i_x")
         load_weight("i_h")
-        load_activations(3)
+        for u in range(3, LOADED):
+            load_activations(u)
         load_m_prev(0)
-        load_m_prev(1)
 
+        neg_bf = keep.tile([P, OUT_CHUNKS], F32, name="neg_bf")
+        bias_i = keep.tile([P, FEAT], F32, name="bias_i")
         transpose_in(0)
         bf_T = sbanks.tile([P, P], BF16, name="bf_T", tag="sbank")
         nc.tensor.transpose(out=bf_T[:], in_=bf_rows[:], identity=ident_bf16[:])
-        neg_bf = keep.tile([P, OUT_CHUNKS], F32, name="neg_bf")
-        bias_i = keep.tile([P, FEAT], F32, name="bias_i")
-
         nc.vector.tensor_scalar_mul(out=neg_bf[:], in0=bf_T[:, 0:OUT_CHUNKS], scalar1=-1.0)
+
         quantise(0, "x")
         quantise(0, "h")
         transpose_in(1)
@@ -281,37 +298,68 @@ def tile_slstmlayer_pa_t_kernel(
         quantise(1, "x")
         quantise(1, "h")
         ln_done = 0
-        for s in range(N_UNITS + LAG + 1):
-            middle = s - LAG
-            last = middle - 1
+        ln_done = 0
+        diff_step = {}
+        step = 0
+        first = 0
+        for end in RUN_ENDS:
+            step = max(step, end + 1)
+            for u in range(first, end + 1):
+                diff_step[step] = u
+                step += 1
+            first = end + 1
+        fin_wait = []
+        m_order = sorted(diff_step)
+        for s in range(step + 1):
+            middle = diff_step.get(s, -1)
             if s + LOADED < N_UNITS:
                 load_activations(s + LOADED)
-            if 2 <= middle + 3 < N_UNITS:
-                load_m_prev(middle + 3)
+            for key in m_order:
+                if key == s + M_AHEAD and diff_step[key] > 0:
+                    load_m_prev(diff_step[key])
             if s < N_UNITS:
                 forget_exp(s)
-            if 0 <= last < N_UNITS:
-                for half in halves:
-                    split_difference(last, half)
-                    final_exp(last, half)
+            late_stores = [] if s - 1 in POST else None
+            for u, half in fin_wait:
+                split_difference(u, half)
+                if s not in LN_FIRST:
+                    final_exp(u, half, late_stores)
+            fin_now = fin_wait
+            fin_wait = []
             if s < N_UNITS:
                 clamp(s)
             if middle == 0:
                 bi_sum = vbanks.tile([P, FEAT], F32, name="bi_sum", tag="vbank")
                 nc.tensor.matmul(out=bi_sum[:], lhsT=ones[:], rhs=bi_row[:], start=True, stop=True)
                 nc.vector.tensor_copy(out=bias_i[:], in_=bi_sum[:])
-            if s + 2 < N_UNITS:
-                transpose_in(s + 2)
-            if 0 <= middle < N_UNITS:
-                input_gate(middle)
+            for work in ORDER.get(s, "AIDQF"):
+                if work == "A" and s + 2 < N_UNITS:
+                    transpose_in(s + 2)
+                if work == "I" and middle >= 0 and "gate" not in tiles[middle]:
+                    input_gate(middle)
+                if work == "D" and middle >= 0:
+                    for half in halves:
+                        difference(middle, range(half.start, half.stop))
+                if work == "Q" and s + 2 < N_UNITS:
+                    quantise(s + 2, "x")
+                    quantise(s + 2, "h")
+                if work == "F" and s + 1 < N_UNITS:
+                    forget_gate(s + 1)
+            for target, part in late_stores or ():
+                nc.sync.dma_start(out=target, in_=part)
+            if middle >= 0:
                 for half in halves:
-                    difference(middle, range(half.start, half.stop))
-            if s + 2 < N_UNITS:
-                quantise(s + 2, "x")
-                quantise(s + 2, "h")
-            if s + 1 < N_UNITS:
-                forget_gate(s + 1)
+                    if middle >= LATE or (middle >= 0 and SAME):
+                        split_difference(middle, half)
+                        final_exp(middle, half)
+                    else:
+                        fin_wait.append((middle, half))
+            for u in EARLY_I.get(s, ()):
+                input_gate(u)
             if s in RUN_ENDS:
                 for u in range(ln_done, s + 1):
                     log(u)
                 ln_done = s + 1
+            if s in LN_FIRST:
+                for u, half in fin_now:
+                    final_exp(u, half)

@@ -23,14 +23,21 @@ OUT_CHUNKS = FEAT // P
 WORDS = FEAT // 2
 RUN_ENDS = (1, 3, 5, 7)
 BIG = 3.0e38
-SAME = False
-ORDER = {0: "FAQ", 1: "IADQF", 2: "IDFAQ", 3: "IADQF", 4: "IDFAQ", 5: "IADQF", 6: "IDFAQ", 7: "IADQF"}
+HALF_LATE = -1
+X_FIRST = (0,)
+AH = 2
+I_AT = 4
+M_BUFS = 4
+G_MAX = ()
+WEAVE = (8,)
+HALVED = 0
+ORDER = {0: "AFQ", 1: "IADQF", 2: "IDFAQ", 3: "IADQF", 4: "IDFAQ", 5: "IADQF", 6: "IDFAQ", 7: "IADQF"}
 LN_FIRST = ()
-EARLY_I = {7: (6, 7)}
-POST = (1, 3, 5)
+EARLY_I = {}
+POST = (1, 3, 5, 7)
 M_AHEAD = 3
 LATE = 6
-HEAD = 0
+HEAD = "0bx1h"
 WARM = 0
 LOADED = 4
 
@@ -66,10 +73,12 @@ def tile_slstmlayer_pa_t_kernel(
     with ExitStack() as stack:
         keep = stack.enter_context(tc.tile_pool(name="keep", bufs=1))
         loads = stack.enter_context(tc.tile_pool(name="loads", bufs=LOADED))
+        m_pool = stack.enter_context(tc.tile_pool(name="m_pool", bufs=M_BUFS))
         regroup = stack.enter_context(tc.tile_pool(name="regroup", bufs=2))
         quant = stack.enter_context(tc.tile_pool(name="quant", bufs=QUANT_BUFS))
         soft_pool = stack.enter_context(tc.tile_pool(name="soft_pool", bufs=SOFT_BUFS))
         gate_pool = stack.enter_context(tc.tile_pool(name="gate_pool", bufs=GATE_BUFS))
+        outs = stack.enter_context(tc.tile_pool(name="outs", bufs=3))
         short = stack.enter_context(tc.tile_pool(name="short", bufs=SHORT_BUFS))
         vbanks = stack.enter_context(tc.psum_pool(name="vbanks", bufs=VBANKS))
         sbanks = stack.enter_context(tc.psum_pool(name="sbanks", bufs=8 - VBANKS))
@@ -87,6 +96,10 @@ def tile_slstmlayer_pa_t_kernel(
         weight_names = ("f_x", "f_h", "i_x", "i_h")
         weight_words = {"f_x": Wf_x_words, "f_h": Wf_h_words, "i_x": Wi_x_words, "i_h": Wi_h_words}
         weight_scales = {"f_x": Wf_x_scales, "f_h": Wf_h_scales, "i_x": Wi_x_scales, "i_h": Wi_h_scales}
+        ones = keep.tile([P, P], BF16, name="ones")
+        nc.vector.memset(ones[:], 1.0)
+        bi_row = keep.tile([P, FEAT], BF16, name="bi_row")
+        nc.vector.memset(bi_row[:], 0.0)
         planes = keep.tile([P, len(weight_names), FEAT], U8, name="planes", align_bytes=64)
         nc.vector.memset(planes[:].rearrange("p w n -> p (w n)").bitcast(I32), 0)
         bf_rows = keep.tile([P, P], BF16, name="bf_rows")
@@ -94,10 +107,6 @@ def tile_slstmlayer_pa_t_kernel(
         warm = keep.tile([P, 1], F32, name="warm")
         nc.vector.memset(warm[:], 0.0)
         nc.scalar.activation(out=warm[:], in_=warm[:], func=ACT.Exp)
-        bi_row = keep.tile([P, FEAT], BF16, name="bi_row")
-        nc.vector.memset(bi_row[:], 0.0)
-        ones = keep.tile([P, P], BF16, name="ones")
-        nc.vector.memset(ones[:], 1.0)
         neg_ident = keep.tile([P, P], BF16, name="neg_ident")
         nc.vector.tensor_scalar_mul(out=neg_ident[:], in0=ident_bf16[:], scalar1=-1.0)
 
@@ -120,30 +129,34 @@ def tile_slstmlayer_pa_t_kernel(
             return planes[:, weight_names.index(w), :]
 
         tiles = {}
+        m_tiles = {}
         halves = (slice(0, ROW_TILES // 2), slice(ROW_TILES // 2, ROW_TILES))
         whole = slice(0, ROW_TILES)
 
         def flat(view):
             return view.rearrange("p j n -> p (j n)")
 
-        def load_activations(u):
-            tiles[u] = {}
-            for name, tensor in (("x", x), ("h", h_prev)):
-                rows = loads.tile([P, ROW_TILES, FEAT], BF16, name=name + "_rows")
-                nc.sync.dma_start(out=rows[:], in_=unit_view(tensor, u))
-                tiles[u][name] = rows
+        def load_activations(u, parts=(whole,), names=("x", "h")):
+            tiles.setdefault(u, {})
+            for part in parts:
+                for name in names:
+                    tensor = {"x": x, "h": h_prev}[name]
+                    if name not in tiles[u]:
+                        tiles[u][name] = loads.tile([P, ROW_TILES, FEAT], BF16, name=name + "_rows")
+                    nc.sync.dma_start(out=tiles[u][name][:, part, :], in_=unit_view(tensor, u)[:, part, :])
 
         def load_m_prev(u):
-            rows = loads.tile([P, ROW_TILES, FEAT], BF16, name="m_rows")
+            rows = m_pool.tile([P, ROW_TILES, FEAT], BF16, name="m_rows")
             nc.sync.dma_start(out=rows[:], in_=unit_view(m_prev, u))
-            tiles[u]["m"] = rows
+            m_tiles[u] = rows
 
-        def transpose_in(u):
-            for n, name in enumerate(("x", "h")):
+        def transpose_in(u, names=("x", "h"), pairs=(0, 1)):
+            for name in names:
                 row_words = tiles[u][name][:].rearrange("p j k -> p (j k)").bitcast(F32)
-                grouped = regroup.tile([P, 4 * UNIT_ROWS], BF16, name=name + "_grouped", align_bytes=64)
-                grouped_words = grouped[:].bitcast(F32).rearrange("p (c v) -> p c v", v=2)
-                for pair in range(ROW_TILES // 2):
+                if name + "_grouped" not in tiles[u]:
+                    tiles[u][name + "_grouped"] = regroup.tile([P, 4 * UNIT_ROWS], BF16, name=name + "_grouped", align_bytes=64)
+                grouped_words = tiles[u][name + "_grouped"][:].bitcast(F32).rearrange("p (c v) -> p c v", v=2)
+                for pair in pairs:
                     bank = vbanks.tile([P, 2, 2, P], F32, name="words_T", tag="vbank")
                     for jj in range(2):
                         first = (2 * pair + jj) * WORDS
@@ -157,7 +170,6 @@ def tile_slstmlayer_pa_t_kernel(
                         "p (jj r) v -> p jj r v", jj=2
                     )
                     nc.vector.tensor_copy(out=target, in_=bank[:].rearrange("p jj v r -> p jj r v"))
-                tiles[u][name + "_grouped"] = grouped
 
         def quantise(u, name):
             codes = quant.tile([P, UNIT_ROWS], U32, name=name + "_codes", align_bytes=64)
@@ -171,19 +183,30 @@ def tile_slstmlayer_pa_t_kernel(
         def forget_gate(u):
             t = tiles[u]
             t["f_T"] = []
-            for c in range(OUT_CHUNKS):
-                acc = sbanks.tile([P, UNIT_ROWS], F32, name="f_T", tag="sbank")
-                for name, first in (("x", True), ("h", False)):
-                    nc.tensor.matmul_mx(
-                        out=acc[:],
-                        lhsT=words["f_" + name][:, 2 * c * P : 2 * (c + 1) * P].bitcast(FP4X4),
-                        lhsT_scale=weight_plane("f_" + name)[:, c * P : (c + 1) * P],
-                        rhs=t[name + "_codes"][:].bitcast(FP8X4),
-                        rhs_scale=t[name + "_scales"][:],
-                        start=first,
-                        stop=not first,
-                    )
-                t["f_T"].append(acc)
+
+            def one_pass(c, name, first):
+                if first:
+                    acc = sbanks.tile([P, UNIT_ROWS], F32, name="f_T", tag="sbank")
+                    t["f_T"].append(acc)
+                nc.tensor.matmul_mx(
+                    out=t["f_T"][c][:],
+                    lhsT=words["f_" + name][:, 2 * c * P : 2 * (c + 1) * P].bitcast(FP4X4),
+                    lhsT_scale=weight_plane("f_" + name)[:, c * P : (c + 1) * P],
+                    rhs=t[name + "_codes"][:].bitcast(FP8X4),
+                    rhs_scale=t[name + "_scales"][:],
+                    start=first,
+                    stop=not first,
+                )
+
+            if u in X_FIRST:
+                for c in range(OUT_CHUNKS):
+                    one_pass(c, "x", True)
+                for c in range(OUT_CHUNKS):
+                    one_pass(c, "h", False)
+            else:
+                for c in range(OUT_CHUNKS):
+                    one_pass(c, "x", True)
+                    one_pass(c, "h", False)
 
         def forget_exp(u):
             t = tiles[u]
@@ -231,7 +254,7 @@ def tile_slstmlayer_pa_t_kernel(
             banks = []
             for j in row_tiles:
                 bank = vbanks.tile([P, FEAT], F32, name="s_minus_m", tag="vbank")
-                nc.tensor.matmul(out=bank[:], lhsT=neg_ident[:], rhs=t["m"][:, j, :], start=True, stop=False)
+                nc.tensor.matmul(out=bank[:], lhsT=neg_ident[:], rhs=m_tiles[u][:, j, :], start=True, stop=False)
                 banks.append(bank)
             for j, bank in zip(row_tiles, banks):
                 for c in range(OUT_CHUNKS):
@@ -245,6 +268,8 @@ def tile_slstmlayer_pa_t_kernel(
                     )
                 i_rows = t["gate"][:, j, :]
                 nc.vector.tensor_tensor(out=t["diff"][:, j, :], in0=bank[:], in1=i_rows, op=ALU.add)
+                if (u, j // 2) in G_MAX:
+                    continue
                 nc.vector.scalar_tensor_tensor(
                     out=i_rows, in0=bank[:], scalar=-1.0, in1=i_rows, op0=ALU.mult, op1=ALU.max
                 )
@@ -258,42 +283,76 @@ def tile_slstmlayer_pa_t_kernel(
             nc.gpsimd.tensor_scalar(out=below, in0=d, scalar1=0.0, scalar2=-BIG, op0=ALU.min, op1=ALU.max)
             nc.gpsimd.tensor_scalar(out=d, in0=d, scalar1=BIG, scalar2=0.0, op0=ALU.min, op1=ALU.max)
 
+        def gpsimd_maximum(u):
+            for half in halves:
+                if (u, half.start // 2) in G_MAX:
+                    gate = flat(tiles[u]["gate"][:, half, :])
+                    nc.gpsimd.tensor_tensor(out=gate, in0=gate, in1=flat(tiles[u]["below"][:, half, :]), op=ALU.subtract)
+                    nc.sync.dma_start(out=unit_view(out_0, u)[:, half, :], in_=tiles[u]["gate"][:, half, :])
+
         def final_exp(u, half, late_stores=None):
             t = tiles[u]
             for name, scale, tensor in (("below", 1.0, out_1), ("diff", -1.0, out_2)):
-                part = t[name][:, half, :]
-                nc.scalar.activation(out=flat(part), in_=flat(part), func=ACT.Exp, scale=scale)
+                source = t[name][:, half, :]
+                part = source
+                if name == "below" and (u, half.start // 2) in G_MAX:
+                    i_out = outs.tile([P, ROW_TILES // 2, FEAT], F32, name="i_out")
+                    part = i_out[:]
+                nc.scalar.activation(out=flat(part), in_=flat(source), func=ACT.Exp, scale=scale)
                 if late_stores is None:
                     nc.sync.dma_start(out=unit_view(tensor, u)[:, half, :], in_=part)
                 else:
                     late_stores.append((unit_view(tensor, u)[:, half, :], part))
 
-        load_activations(0)
-        nc.sync.dma_start(out=bf_rows[0:OUT_CHUNKS, :], in_=b_f.rearrange("(c n) -> c n", c=OUT_CHUNKS))
-        if HEAD == 0:
-            load_activations(1)
-        load_weight("f_x")
-        load_weight("f_h")
-        if HEAD == 1:
-            load_activations(1)
-        load_activations(2)
-        nc.sync.dma_start(out=bi_row[0:1, :], in_=b_i.rearrange("(o n) -> o n", o=1))
-        load_weight("i_x")
-        load_weight("i_h")
-        for u in range(3, LOADED):
+        def load_bf():
+            nc.sync.dma_start(out=bf_rows[0:OUT_CHUNKS, :], in_=b_f.rearrange("(c n) -> c n", c=OUT_CHUNKS))
+
+        for what in HEAD:
+            if what == "0":
+                load_activations(0, halves if HALVED > 0 else (whole,))
+            if what == "1":
+                load_activations(1, halves if HALVED > 1 else (whole,))
+            if what == "x":
+                load_weight("f_x")
+            if what == "h":
+                load_weight("f_h")
+            if what == "b":
+                load_bf()
+            if what == "p":
+                load_activations(1, names=("x",))
+            if what == "q":
+                load_activations(1, names=("h",))
+        def load_input_gate():
+            nc.sync.dma_start(out=bi_row[0:1, :], in_=b_i.rearrange("(o n) -> o n", o=1))
+            load_weight("i_x")
+            load_weight("i_h")
+
+        for u in range(2, LOADED):
+            if I_AT == u:
+                load_input_gate()
             load_activations(u)
+        if I_AT == LOADED:
+            load_input_gate()
         load_m_prev(0)
 
         neg_bf = keep.tile([P, OUT_CHUNKS], F32, name="neg_bf")
         bias_i = keep.tile([P, FEAT], F32, name="bias_i")
-        transpose_in(0)
+        if HALVED > 0:
+            transpose_in(0, pairs=(0,))
+            transpose_in(0, pairs=(1,))
+        else:
+            transpose_in(0)
         bf_T = sbanks.tile([P, P], BF16, name="bf_T", tag="sbank")
         nc.tensor.transpose(out=bf_T[:], in_=bf_rows[:], identity=ident_bf16[:])
         nc.vector.tensor_scalar_mul(out=neg_bf[:], in0=bf_T[:, 0:OUT_CHUNKS], scalar1=-1.0)
 
         quantise(0, "x")
         quantise(0, "h")
-        transpose_in(1)
+        if HALVED > 1:
+            transpose_in(1, pairs=(0,))
+            transpose_in(1, pairs=(1,))
+        else:
+            transpose_in(1)
         forget_gate(0)
         quantise(1, "x")
         quantise(1, "h")
@@ -315,7 +374,7 @@ def tile_slstmlayer_pa_t_kernel(
             if s + LOADED < N_UNITS:
                 load_activations(s + LOADED)
             for key in m_order:
-                if key == s + M_AHEAD and diff_step[key] > 0:
+                if key <= s + M_AHEAD and diff_step[key] not in m_tiles:
                     load_m_prev(diff_step[key])
             if s < N_UNITS:
                 forget_exp(s)
@@ -328,28 +387,34 @@ def tile_slstmlayer_pa_t_kernel(
             fin_wait = []
             if s < N_UNITS:
                 clamp(s)
+            for u in sorted({u for u, half in fin_now}):
+                gpsimd_maximum(u)
             if middle == 0:
                 bi_sum = vbanks.tile([P, FEAT], F32, name="bi_sum", tag="vbank")
                 nc.tensor.matmul(out=bi_sum[:], lhsT=ones[:], rhs=bi_row[:], start=True, stop=True)
                 nc.vector.tensor_copy(out=bias_i[:], in_=bi_sum[:])
             for work in ORDER.get(s, "AIDQF"):
-                if work == "A" and s + 2 < N_UNITS:
-                    transpose_in(s + 2)
+                if work == "A" and 2 <= s + AH < N_UNITS:
+                    transpose_in(s + AH)
                 if work == "I" and middle >= 0 and "gate" not in tiles[middle]:
                     input_gate(middle)
                 if work == "D" and middle >= 0:
                     for half in halves:
                         difference(middle, range(half.start, half.stop))
-                if work == "Q" and s + 2 < N_UNITS:
-                    quantise(s + 2, "x")
-                    quantise(s + 2, "h")
+                        if s in WEAVE:
+                            for target, part in late_stores[:2]:
+                                nc.sync.dma_start(out=target, in_=part)
+                            late_stores = late_stores[2:]
+                if work == "Q" and 2 <= s + AH < N_UNITS:
+                    quantise(s + AH, "x")
+                    quantise(s + AH, "h")
                 if work == "F" and s + 1 < N_UNITS:
                     forget_gate(s + 1)
             for target, part in late_stores or ():
                 nc.sync.dma_start(out=target, in_=part)
             if middle >= 0:
                 for half in halves:
-                    if middle >= LATE or (middle >= 0 and SAME):
+                    if middle >= LATE or (middle == HALF_LATE and half == halves[0]):
                         split_difference(middle, half)
                         final_exp(middle, half)
                     else:

@@ -24,17 +24,23 @@ WORDS = FEAT // 2
 RUN_ENDS = (1, 3, 5, 7)
 BIG = 3.0e38
 HALF_LATE = -1
+F_FIRST = True
+CLAMP_CHUNKS = 2
+V_CLAMP = ()
+V_SPLIT = ()
+WHOLE_SPLIT = ()
 X_FIRST = (0,)
 AH = 2
+LOAD_AT = ((4, 0), (5, 1), (6, 2), (7, 3))
 I_AT = 4
 M_BUFS = 4
 G_MAX = ()
-WEAVE = (8,)
+WEAVE = ()
 HALVED = 0
 ORDER = {0: "AFQ", 1: "IADQF", 2: "IDFAQ", 3: "IADQF", 4: "IDFAQ", 5: "IADQF", 6: "IDFAQ", 7: "IADQF"}
 LN_FIRST = ()
 EARLY_I = {}
-POST = (1, 3, 5, 7)
+POST = (7,)
 M_AHEAD = 3
 LATE = 6
 HEAD = "0bx1h"
@@ -42,7 +48,7 @@ WARM = 0
 LOADED = 4
 
 SOFT_BUFS = 4
-GATE_BUFS = 3
+GATE_BUFS = 4
 SHORT_BUFS = 3
 VBANKS = 4
 QUANT_BUFS = 6
@@ -218,9 +224,12 @@ def tile_slstmlayer_pa_t_kernel(
             t["soft_T"] = soft
 
         def clamp(u):
-            for c in range(0, OUT_CHUNKS, 2):
-                part = flat(tiles[u]["soft_T"][:, c : c + 2, :])
-                nc.gpsimd.tensor_scalar(out=part, in0=part, scalar1=1.0e8 - 1.0, scalar2=0.0, op0=ALU.min, op1=ALU.max)
+            for c in range(0, OUT_CHUNKS, CLAMP_CHUNKS):
+                part = flat(tiles[u]["soft_T"][:, c : c + CLAMP_CHUNKS, :])
+                if u in V_CLAMP:
+                    nc.vector.tensor_scalar_min(out=part, in0=part, scalar1=1.0e8 - 1.0)
+                else:
+                    nc.gpsimd.tensor_scalar(out=part, in0=part, scalar1=1.0e8 - 1.0, scalar2=0.0, op0=ALU.min, op1=ALU.max)
 
         def log(u):
             soft = tiles[u]["soft_T"]
@@ -246,11 +255,11 @@ def tile_slstmlayer_pa_t_kernel(
                 nc.vector.tensor_tensor(out=gate[:, j, :], in0=acc[:], in1=bias_i[:], op=ALU.add)
             t["gate"] = gate
 
-        def difference(u, row_tiles):
+        def new_maximum(u, row_tiles):
             t = tiles[u]
-            if "diff" not in t:
-                t["diff"] = short.tile([P, ROW_TILES, FEAT], F32, name="diff")
-                t["below"] = short.tile([P, ROW_TILES, FEAT], F32, name="below")
+            if "m_new" not in t:
+                t["m_new"] = short.tile([P, ROW_TILES, FEAT], F32, name="m_new")
+                t["over"] = short.tile([P, ROW_TILES, FEAT], F32, name="over")
             banks = []
             for j in row_tiles:
                 bank = vbanks.tile([P, FEAT], F32, name="s_minus_m", tag="vbank")
@@ -266,39 +275,30 @@ def tile_slstmlayer_pa_t_kernel(
                         start=False,
                         stop=(c == OUT_CHUNKS - 1),
                     )
-                i_rows = t["gate"][:, j, :]
-                nc.vector.tensor_tensor(out=t["diff"][:, j, :], in0=bank[:], in1=i_rows, op=ALU.add)
-                if (u, j // 2) in G_MAX:
-                    continue
                 nc.vector.scalar_tensor_tensor(
-                    out=i_rows, in0=bank[:], scalar=-1.0, in1=i_rows, op0=ALU.mult, op1=ALU.max
+                    out=t["m_new"][:, j, :], in0=bank[:], scalar=-1.0, in1=t["gate"][:, j, :], op0=ALU.mult, op1=ALU.max
                 )
-                if j % 2 == 1:
-                    half = halves[j // 2]
-                    nc.sync.dma_start(out=unit_view(out_0, u)[:, half, :], in_=t["gate"][:, half, :])
+            half = slice(row_tiles.start, row_tiles.stop)
+            nc.sync.dma_start(out=unit_view(out_0, u)[:, half, :], in_=t["m_new"][:, half, :])
+            for j, bank in zip(row_tiles, banks):
+                nc.vector.tensor_tensor(out=t["over"][:, j, :], in0=bank[:], in1=t["m_new"][:, j, :], op=ALU.add)
 
-        def split_difference(u, half):
-            d = flat(tiles[u]["diff"][:, half, :])
-            below = flat(tiles[u]["below"][:, half, :])
-            nc.gpsimd.tensor_scalar(out=below, in0=d, scalar1=0.0, scalar2=-BIG, op0=ALU.min, op1=ALU.max)
-            nc.gpsimd.tensor_scalar(out=d, in0=d, scalar1=BIG, scalar2=0.0, op0=ALU.min, op1=ALU.max)
+        def input_exponent(u, half):
+            gate = flat(tiles[u]["gate"][:, half, :])
+            engine = nc.vector if (u, half.start // 2) in V_SPLIT else nc.gpsimd
+            engine.tensor_tensor(out=gate, in0=gate, in1=flat(tiles[u]["m_new"][:, half, :]), op=ALU.subtract)
 
-        def gpsimd_maximum(u):
-            for half in halves:
-                if (u, half.start // 2) in G_MAX:
-                    gate = flat(tiles[u]["gate"][:, half, :])
-                    nc.gpsimd.tensor_tensor(out=gate, in0=gate, in1=flat(tiles[u]["below"][:, half, :]), op=ALU.subtract)
-                    nc.sync.dma_start(out=unit_view(out_0, u)[:, half, :], in_=tiles[u]["gate"][:, half, :])
-
-        def final_exp(u, half, late_stores=None):
+        def final_exp(u, parts, late_stores=None):
             t = tiles[u]
-            for name, scale, tensor in (("below", 1.0, out_1), ("diff", -1.0, out_2)):
-                source = t[name][:, half, :]
-                part = source
-                if name == "below" and (u, half.start // 2) in G_MAX:
-                    i_out = outs.tile([P, ROW_TILES // 2, FEAT], F32, name="i_out")
-                    part = i_out[:]
-                nc.scalar.activation(out=flat(part), in_=flat(source), func=ACT.Exp, scale=scale)
+            order = []
+            if F_FIRST:
+                order = [("over", -1.0, out_2, half) for half in parts] + [("gate", 1.0, out_1, half) for half in parts]
+            else:
+                for half in parts:
+                    order += [("over", -1.0, out_2, half), ("gate", 1.0, out_1, half)]
+            for name, scale, tensor, half in order:
+                part = t[name][:, half, :]
+                nc.scalar.activation(out=flat(part), in_=flat(part), func=ACT.Exp, scale=scale)
                 if late_stores is None:
                     nc.sync.dma_start(out=unit_view(tensor, u)[:, half, :], in_=part)
                 else:
@@ -371,8 +371,9 @@ def tile_slstmlayer_pa_t_kernel(
         m_order = sorted(diff_step)
         for s in range(step + 1):
             middle = diff_step.get(s, -1)
-            if s + LOADED < N_UNITS:
-                load_activations(s + LOADED)
+            for u, step_of_load in LOAD_AT:
+                if step_of_load == s:
+                    load_activations(u)
             for key in m_order:
                 if key <= s + M_AHEAD and diff_step[key] not in m_tiles:
                     load_m_prev(diff_step[key])
@@ -380,15 +381,12 @@ def tile_slstmlayer_pa_t_kernel(
                 forget_exp(s)
             late_stores = [] if s - 1 in POST else None
             for u, half in fin_wait:
-                split_difference(u, half)
-                if s not in LN_FIRST:
-                    final_exp(u, half, late_stores)
-            fin_now = fin_wait
+                input_exponent(u, half)
+            if fin_wait:
+                final_exp(fin_wait[0][0], [half for u, half in fin_wait], late_stores)
             fin_wait = []
             if s < N_UNITS:
                 clamp(s)
-            for u in sorted({u for u, half in fin_now}):
-                gpsimd_maximum(u)
             if middle == 0:
                 bi_sum = vbanks.tile([P, FEAT], F32, name="bi_sum", tag="vbank")
                 nc.tensor.matmul(out=bi_sum[:], lhsT=ones[:], rhs=bi_row[:], start=True, stop=True)
@@ -400,7 +398,7 @@ def tile_slstmlayer_pa_t_kernel(
                     input_gate(middle)
                 if work == "D" and middle >= 0:
                     for half in halves:
-                        difference(middle, range(half.start, half.stop))
+                        new_maximum(middle, range(half.start, half.stop))
                         if s in WEAVE:
                             for target, part in late_stores[:2]:
                                 nc.sync.dma_start(out=target, in_=part)
@@ -415,8 +413,8 @@ def tile_slstmlayer_pa_t_kernel(
             if middle >= 0:
                 for half in halves:
                     if middle >= LATE or (middle == HALF_LATE and half == halves[0]):
-                        split_difference(middle, half)
-                        final_exp(middle, half)
+                        input_exponent(middle, half)
+                        final_exp(middle, [half])
                     else:
                         fin_wait.append((middle, half))
             for u in EARLY_I.get(s, ()):
@@ -425,6 +423,3 @@ def tile_slstmlayer_pa_t_kernel(
                 for u in range(ln_done, s + 1):
                     log(u)
                 ln_done = s + 1
-            if s in LN_FIRST:
-                for u, half in fin_now:
-                    final_exp(u, half)

@@ -24,7 +24,8 @@ WORDS = FEAT // 2
 RUN_ENDS = (1, 3, 5, 7)
 BIG = 3.0e38
 HALF_LATE = -1
-F_FIRST = True
+S_COPIES = ()
+DEFER = (3,)
 CLAMP_CHUNKS = 2
 V_CLAMP = ()
 V_SPLIT = ()
@@ -175,7 +176,10 @@ def tile_slstmlayer_pa_t_kernel(
                     target = grouped_words[:, 2 * pair * P : (2 * pair + 2) * P, :].rearrange(
                         "p (jj r) v -> p jj r v", jj=2
                     )
-                    nc.vector.tensor_copy(out=target, in_=bank[:].rearrange("p jj v r -> p jj r v"))
+                    if (u, name, pair) in S_COPIES:
+                        nc.scalar.copy(out=target, in_=bank[:].rearrange("p jj v r -> p jj r v"))
+                    else:
+                        nc.vector.tensor_copy(out=target, in_=bank[:].rearrange("p jj v r -> p jj r v"))
 
         def quantise(u, name):
             codes = quant.tile([P, UNIT_ROWS], U32, name=name + "_codes", align_bytes=64)
@@ -288,21 +292,19 @@ def tile_slstmlayer_pa_t_kernel(
             engine = nc.vector if (u, half.start // 2) in V_SPLIT else nc.gpsimd
             engine.tensor_tensor(out=gate, in0=gate, in1=flat(tiles[u]["m_new"][:, half, :]), op=ALU.subtract)
 
-        def final_exp(u, parts, late_stores=None):
-            t = tiles[u]
-            order = []
-            if F_FIRST:
-                order = [("over", -1.0, out_2, half) for half in parts] + [("gate", 1.0, out_1, half) for half in parts]
+        def exp_and_store(u, name, scale, tensor, half, late_stores):
+            part = tiles[u][name][:, half, :]
+            nc.scalar.activation(out=flat(part), in_=flat(part), func=ACT.Exp, scale=scale)
+            if late_stores is None:
+                nc.sync.dma_start(out=unit_view(tensor, u)[:, half, :], in_=part)
             else:
-                for half in parts:
-                    order += [("over", -1.0, out_2, half), ("gate", 1.0, out_1, half)]
-            for name, scale, tensor, half in order:
-                part = t[name][:, half, :]
-                nc.scalar.activation(out=flat(part), in_=flat(part), func=ACT.Exp, scale=scale)
-                if late_stores is None:
-                    nc.sync.dma_start(out=unit_view(tensor, u)[:, half, :], in_=part)
-                else:
-                    late_stores.append((unit_view(tensor, u)[:, half, :], part))
+                late_stores.append((unit_view(tensor, u)[:, half, :], part))
+
+        def forget_final(u, half, late_stores=None):
+            exp_and_store(u, "over", -1.0, out_2, half, late_stores)
+
+        def input_final(u, half, late_stores=None):
+            exp_and_store(u, "gate", 1.0, out_1, half, late_stores)
 
         def load_bf():
             nc.sync.dma_start(out=bf_rows[0:OUT_CHUNKS, :], in_=b_f.rearrange("(c n) -> c n", c=OUT_CHUNKS))
@@ -380,13 +382,24 @@ def tile_slstmlayer_pa_t_kernel(
             if s < N_UNITS:
                 forget_exp(s)
             late_stores = [] if s - 1 in POST else None
+            deferred = []
             for u, half in fin_wait:
-                input_exponent(u, half)
+                if s in DEFER and half == halves[1]:
+                    deferred.append((u, half))
+                else:
+                    input_exponent(u, half)
             if fin_wait:
-                final_exp(fin_wait[0][0], [half for u, half in fin_wait], late_stores)
+                u = fin_wait[0][0]
+                for half in halves:
+                    forget_final(u, half, late_stores)
+                for u, half in fin_wait:
+                    if (u, half) not in deferred:
+                        input_final(u, half, late_stores)
             fin_wait = []
             if s < N_UNITS:
                 clamp(s)
+            for u, half in deferred:
+                input_exponent(u, half)
             if middle == 0:
                 bi_sum = vbanks.tile([P, FEAT], F32, name="bi_sum", tag="vbank")
                 nc.tensor.matmul(out=bi_sum[:], lhsT=ones[:], rhs=bi_row[:], start=True, stop=True)
@@ -414,7 +427,8 @@ def tile_slstmlayer_pa_t_kernel(
                 for half in halves:
                     if middle >= LATE or (middle == HALF_LATE and half == halves[0]):
                         input_exponent(middle, half)
-                        final_exp(middle, [half])
+                        forget_final(middle, half)
+                        input_final(middle, half)
                     else:
                         fin_wait.append((middle, half))
             for u in EARLY_I.get(s, ()):
@@ -423,3 +437,5 @@ def tile_slstmlayer_pa_t_kernel(
                 for u in range(ln_done, s + 1):
                     log(u)
                 ln_done = s + 1
+            for u, half in deferred:
+                input_final(u, half, None)

@@ -21,38 +21,20 @@ UNIT_ROWS = P * ROW_TILES
 N_UNITS = BATCH // UNIT_ROWS
 OUT_CHUNKS = FEAT // P
 WORDS = FEAT // 2
-RUN_ENDS = (1, 3, 5, 7)
-BIG = 3.0e38
-HALF_LATE = -1
-S_COPIES = ()
-DEFER = (3,)
-CLAMP_CHUNKS = 2
-V_CLAMP = ()
-V_SPLIT = ()
-WHOLE_SPLIT = ()
-X_FIRST = (0,)
-AH = 2
-LOAD_AT = ((4, 0), (5, 1), (6, 2), (7, 3))
-I_AT = 4
-M_BUFS = 4
-G_MAX = ()
-WEAVE = ()
-HALVED = 0
-ORDER = {0: "AFQ", 1: "IADQF", 2: "IDFAQ", 3: "IADQF", 4: "IDFAQ", 5: "IADQF", 6: "IDFAQ", 7: "IADQF"}
-LN_FIRST = ()
-EARLY_I = {}
-POST = (7,)
-M_AHEAD = 3
-LATE = 6
-HEAD = "0bx1h"
-WARM = 0
-LOADED = 4
+QUADRANTS = 4
+HALVES = (range(0, ROW_TILES // 2), range(ROW_TILES // 2, ROW_TILES))
 
+RUN = 2
+LAG = 2
+LATE = N_UNITS - RUN
+
+LOAD_BUFS = 4
+M_BUFS = 4
+QUANT_BUFS = 6
 SOFT_BUFS = 4
 GATE_BUFS = 4
 SHORT_BUFS = 3
 VBANKS = 4
-QUANT_BUFS = 6
 
 FLOPS = 2 * BATCH * FEAT * FEAT * 4
 
@@ -79,13 +61,12 @@ def tile_slstmlayer_pa_t_kernel(
     nc = tc.nc
     with ExitStack() as stack:
         keep = stack.enter_context(tc.tile_pool(name="keep", bufs=1))
-        loads = stack.enter_context(tc.tile_pool(name="loads", bufs=LOADED))
+        loads = stack.enter_context(tc.tile_pool(name="loads", bufs=LOAD_BUFS))
         m_pool = stack.enter_context(tc.tile_pool(name="m_pool", bufs=M_BUFS))
         regroup = stack.enter_context(tc.tile_pool(name="regroup", bufs=2))
         quant = stack.enter_context(tc.tile_pool(name="quant", bufs=QUANT_BUFS))
         soft_pool = stack.enter_context(tc.tile_pool(name="soft_pool", bufs=SOFT_BUFS))
         gate_pool = stack.enter_context(tc.tile_pool(name="gate_pool", bufs=GATE_BUFS))
-        outs = stack.enter_context(tc.tile_pool(name="outs", bufs=3))
         short = stack.enter_context(tc.tile_pool(name="short", bufs=SHORT_BUFS))
         vbanks = stack.enter_context(tc.psum_pool(name="vbanks", bufs=VBANKS))
         sbanks = stack.enter_context(tc.psum_pool(name="sbanks", bufs=8 - VBANKS))
@@ -94,6 +75,9 @@ def tile_slstmlayer_pa_t_kernel(
         def unit_view(tensor, u):
             rows = tensor[u * UNIT_ROWS : (u + 1) * UNIT_ROWS, :]
             return rows.rearrange("(p j) n -> p j n", j=ROW_TILES)
+
+        def half_view(tensor, u, half):
+            return unit_view(tensor, u)[:, half.start : half.stop, :]
 
         ident_f32 = keep.tile([P, P], F32, name="ident_f32")
         make_identity(nc, ident_f32[:])
@@ -111,11 +95,13 @@ def tile_slstmlayer_pa_t_kernel(
         nc.vector.memset(planes[:].rearrange("p w n -> p (w n)").bitcast(I32), 0)
         bf_rows = keep.tile([P, P], BF16, name="bf_rows")
         nc.vector.memset(bf_rows[:], 0.0)
-        warm = keep.tile([P, 1], F32, name="warm")
-        nc.vector.memset(warm[:], 0.0)
-        nc.scalar.activation(out=warm[:], in_=warm[:], func=ACT.Exp)
+        one_column = keep.tile([P, 1], F32, name="one_column")
+        nc.vector.memset(one_column[:], 0.0)
+        nc.scalar.activation(out=one_column[:], in_=one_column[:], func=ACT.Exp)
         neg_ident = keep.tile([P, P], BF16, name="neg_ident")
         nc.vector.tensor_scalar_mul(out=neg_ident[:], in0=ident_bf16[:], scalar1=-1.0)
+        neg_bf = keep.tile([P, OUT_CHUNKS], F32, name="neg_bf")
+        bias_i = keep.tile([P, FEAT], F32, name="bias_i")
 
         words = {}
 
@@ -126,7 +112,7 @@ def tile_slstmlayer_pa_t_kernel(
                 in_=weight_words[w].rearrange("g p b -> (g p) b").bitcast(I32),
             )
             scale_rows = weight_scales[w].rearrange("g q n -> (g q) n")
-            for quad in range(4):
+            for quad in range(QUADRANTS):
                 nc.sync.dma_start(
                     out=planes[32 * quad : 32 * quad + 4, weight_names.index(w), :].bitcast(I32),
                     in_=scale_rows[4 * quad : 4 * quad + 4, :].bitcast(I32),
@@ -135,35 +121,28 @@ def tile_slstmlayer_pa_t_kernel(
         def weight_plane(w):
             return planes[:, weight_names.index(w), :]
 
-        tiles = {}
-        m_tiles = {}
-        halves = (slice(0, ROW_TILES // 2), slice(ROW_TILES // 2, ROW_TILES))
-        whole = slice(0, ROW_TILES)
+        tiles = {u: {} for u in range(N_UNITS)}
 
-        def flat(view):
-            return view.rearrange("p j n -> p (j n)")
-
-        def load_activations(u, parts=(whole,), names=("x", "h")):
-            tiles.setdefault(u, {})
-            for part in parts:
-                for name in names:
-                    tensor = {"x": x, "h": h_prev}[name]
-                    if name not in tiles[u]:
-                        tiles[u][name] = loads.tile([P, ROW_TILES, FEAT], BF16, name=name + "_rows")
-                    nc.sync.dma_start(out=tiles[u][name][:, part, :], in_=unit_view(tensor, u)[:, part, :])
+        def load_activations(u):
+            for name, tensor in (("x", x), ("h", h_prev)):
+                rows = loads.tile([P, ROW_TILES, FEAT], BF16, name=name + "_rows")
+                nc.sync.dma_start(out=rows[:], in_=unit_view(tensor, u))
+                tiles[u][name] = rows
 
         def load_m_prev(u):
             rows = m_pool.tile([P, ROW_TILES, FEAT], BF16, name="m_rows")
             nc.sync.dma_start(out=rows[:], in_=unit_view(m_prev, u))
-            m_tiles[u] = rows
+            tiles[u]["m"] = rows
 
-        def transpose_in(u, names=("x", "h"), pairs=(0, 1)):
-            for name in names:
+        def flat(view):
+            return view.rearrange("p j n -> p (j n)")
+
+        def transpose_in(u):
+            for name in ("x", "h"):
                 row_words = tiles[u][name][:].rearrange("p j k -> p (j k)").bitcast(F32)
-                if name + "_grouped" not in tiles[u]:
-                    tiles[u][name + "_grouped"] = regroup.tile([P, 4 * UNIT_ROWS], BF16, name=name + "_grouped", align_bytes=64)
-                grouped_words = tiles[u][name + "_grouped"][:].bitcast(F32).rearrange("p (c v) -> p c v", v=2)
-                for pair in pairs:
+                grouped = regroup.tile([P, 4 * UNIT_ROWS], BF16, name=name + "_grouped", align_bytes=64)
+                grouped_words = grouped[:].bitcast(F32).rearrange("p (c v) -> p c v", v=2)
+                for pair in range(ROW_TILES // 2):
                     bank = vbanks.tile([P, 2, 2, P], F32, name="words_T", tag="vbank")
                     for jj in range(2):
                         first = (2 * pair + jj) * WORDS
@@ -176,47 +155,38 @@ def tile_slstmlayer_pa_t_kernel(
                     target = grouped_words[:, 2 * pair * P : (2 * pair + 2) * P, :].rearrange(
                         "p (jj r) v -> p jj r v", jj=2
                     )
-                    if (u, name, pair) in S_COPIES:
-                        nc.scalar.copy(out=target, in_=bank[:].rearrange("p jj v r -> p jj r v"))
-                    else:
-                        nc.vector.tensor_copy(out=target, in_=bank[:].rearrange("p jj v r -> p jj r v"))
+                    nc.vector.tensor_copy(out=target, in_=bank[:].rearrange("p jj v r -> p jj r v"))
+                tiles[u][name + "_grouped"] = grouped
 
-        def quantise(u, name):
-            codes = quant.tile([P, UNIT_ROWS], U32, name=name + "_codes", align_bytes=64)
-            scales = quant.tile([P, UNIT_ROWS], U8, name=name + "_scales", align_bytes=64)
-            nc.vector.quantize_mx(
-                out=codes[:].bitcast(FP8X4), scales=scales[:], in_=tiles[u][name + "_grouped"][:]
-            )
-            tiles[u][name + "_codes"] = codes
-            tiles[u][name + "_scales"] = scales
+        def quantise(u):
+            for name in ("x", "h"):
+                codes = quant.tile([P, UNIT_ROWS], U32, name=name + "_codes", align_bytes=64)
+                scales = quant.tile([P, UNIT_ROWS], U8, name=name + "_scales", align_bytes=64)
+                nc.vector.quantize_mx(
+                    out=codes[:].bitcast(FP8X4), scales=scales[:], in_=tiles[u][name + "_grouped"][:]
+                )
+                tiles[u][name + "_codes"] = codes
+                tiles[u][name + "_scales"] = scales
 
         def forget_gate(u):
             t = tiles[u]
-            t["f_T"] = []
-
-            def one_pass(c, name, first):
-                if first:
+            passes = [(c, name) for c in range(OUT_CHUNKS) for name in ("x", "h")]
+            if u == 0:
+                passes = [(c, name) for name in ("x", "h") for c in range(OUT_CHUNKS)]
+            t["f_T"] = {}
+            for c, name in passes:
+                if name == "x":
                     acc = sbanks.tile([P, UNIT_ROWS], F32, name="f_T", tag="sbank")
-                    t["f_T"].append(acc)
+                    t["f_T"][c] = acc
                 nc.tensor.matmul_mx(
                     out=t["f_T"][c][:],
                     lhsT=words["f_" + name][:, 2 * c * P : 2 * (c + 1) * P].bitcast(FP4X4),
                     lhsT_scale=weight_plane("f_" + name)[:, c * P : (c + 1) * P],
                     rhs=t[name + "_codes"][:].bitcast(FP8X4),
                     rhs_scale=t[name + "_scales"][:],
-                    start=first,
-                    stop=not first,
+                    start=(name == "x"),
+                    stop=(name == "h"),
                 )
-
-            if u in X_FIRST:
-                for c in range(OUT_CHUNKS):
-                    one_pass(c, "x", True)
-                for c in range(OUT_CHUNKS):
-                    one_pass(c, "h", False)
-            else:
-                for c in range(OUT_CHUNKS):
-                    one_pass(c, "x", True)
-                    one_pass(c, "h", False)
 
         def forget_exp(u):
             t = tiles[u]
@@ -228,214 +198,173 @@ def tile_slstmlayer_pa_t_kernel(
             t["soft_T"] = soft
 
         def clamp(u):
-            for c in range(0, OUT_CHUNKS, CLAMP_CHUNKS):
-                part = flat(tiles[u]["soft_T"][:, c : c + CLAMP_CHUNKS, :])
-                if u in V_CLAMP:
-                    nc.vector.tensor_scalar_min(out=part, in0=part, scalar1=1.0e8 - 1.0)
-                else:
-                    nc.gpsimd.tensor_scalar(out=part, in0=part, scalar1=1.0e8 - 1.0, scalar2=0.0, op0=ALU.min, op1=ALU.max)
+            for c in range(0, OUT_CHUNKS, 2):
+                part = flat(tiles[u]["soft_T"][:, c : c + 2, :])
+                nc.gpsimd.tensor_scalar(
+                    out=part, in0=part, scalar1=1.0e8 - 1.0, scalar2=0.0, op0=ALU.min, op1=ALU.max
+                )
 
         def log(u):
             soft = tiles[u]["soft_T"]
-            for r in range(2):
-                part = soft[:, :, r * UNIT_ROWS // 2 : (r + 1) * UNIT_ROWS // 2]
+            for half in HALVES:
+                part = soft[:, :, half.start * P : half.stop * P]
                 nc.scalar.activation(out=part, in_=part, func=ACT.Ln, bias=1.0)
+
+        def spread_b_i():
+            bi_sum = vbanks.tile([P, FEAT], F32, name="bi_sum", tag="vbank")
+            nc.tensor.matmul(out=bi_sum[:], lhsT=ones[:], rhs=bi_row[:], start=True, stop=True)
+            nc.vector.tensor_copy(out=bias_i[:], in_=bi_sum[:])
 
         def input_gate(u):
             t = tiles[u]
             gate = gate_pool.tile([P, ROW_TILES, FEAT], F32, name="gate")
             for j in range(ROW_TILES):
                 acc = vbanks.tile([P, FEAT], F32, name="i_rows", tag="vbank")
-                for name, first in (("x", True), ("h", False)):
+                for name in ("x", "h"):
                     nc.tensor.matmul_mx(
                         out=acc[:],
                         lhsT=t[name + "_codes"][:, j * P : (j + 1) * P].bitcast(FP8X4),
                         lhsT_scale=t[name + "_scales"][:, j * P : (j + 1) * P],
                         rhs=words["i_" + name][:].bitcast(FP4X4),
                         rhs_scale=weight_plane("i_" + name),
-                        start=first,
-                        stop=not first,
+                        start=(name == "x"),
+                        stop=(name == "h"),
                     )
                 nc.vector.tensor_tensor(out=gate[:, j, :], in0=acc[:], in1=bias_i[:], op=ALU.add)
             t["gate"] = gate
 
-        def new_maximum(u, row_tiles):
+        def new_maximum(u):
             t = tiles[u]
-            if "m_new" not in t:
-                t["m_new"] = short.tile([P, ROW_TILES, FEAT], F32, name="m_new")
-                t["over"] = short.tile([P, ROW_TILES, FEAT], F32, name="over")
-            banks = []
-            for j in row_tiles:
-                bank = vbanks.tile([P, FEAT], F32, name="s_minus_m", tag="vbank")
-                nc.tensor.matmul(out=bank[:], lhsT=neg_ident[:], rhs=m_tiles[u][:, j, :], start=True, stop=False)
-                banks.append(bank)
-            for j, bank in zip(row_tiles, banks):
-                for c in range(OUT_CHUNKS):
-                    nc.tensor.matmul(
-                        out=bank[:, c * P : (c + 1) * P],
-                        lhsT=t["soft_T"][:, c, j * P : (j + 1) * P],
-                        rhs=ident_f32[:],
-                        is_transpose=True,
-                        start=False,
-                        stop=(c == OUT_CHUNKS - 1),
+            m_new = short.tile([P, ROW_TILES, FEAT], F32, name="m_new")
+            over = short.tile([P, ROW_TILES, FEAT], F32, name="over")
+            for half in HALVES:
+                banks = {}
+                for j in half:
+                    bank = vbanks.tile([P, FEAT], F32, name="s_minus_m", tag="vbank")
+                    nc.tensor.matmul(out=bank[:], lhsT=neg_ident[:], rhs=t["m"][:, j, :], start=True, stop=False)
+                    banks[j] = bank
+                for j in half:
+                    for c in range(OUT_CHUNKS):
+                        nc.tensor.matmul(
+                            out=banks[j][:, c * P : (c + 1) * P],
+                            lhsT=t["soft_T"][:, c, j * P : (j + 1) * P],
+                            rhs=ident_f32[:],
+                            is_transpose=True,
+                            start=False,
+                            stop=(c == OUT_CHUNKS - 1),
+                        )
+                    nc.vector.scalar_tensor_tensor(
+                        out=m_new[:, j, :],
+                        in0=banks[j][:],
+                        scalar=-1.0,
+                        in1=t["gate"][:, j, :],
+                        op0=ALU.mult,
+                        op1=ALU.max,
                     )
-                nc.vector.scalar_tensor_tensor(
-                    out=t["m_new"][:, j, :], in0=bank[:], scalar=-1.0, in1=t["gate"][:, j, :], op0=ALU.mult, op1=ALU.max
-                )
-            half = slice(row_tiles.start, row_tiles.stop)
-            nc.sync.dma_start(out=unit_view(out_0, u)[:, half, :], in_=t["m_new"][:, half, :])
-            for j, bank in zip(row_tiles, banks):
-                nc.vector.tensor_tensor(out=t["over"][:, j, :], in0=bank[:], in1=t["m_new"][:, j, :], op=ALU.add)
+                nc.sync.dma_start(out=half_view(out_0, u, half), in_=m_new[:, half.start : half.stop, :])
+                for j in half:
+                    nc.vector.tensor_tensor(out=over[:, j, :], in0=banks[j][:], in1=m_new[:, j, :], op=ALU.add)
+            t["m_new"] = m_new
+            t["over"] = over
 
         def input_exponent(u, half):
-            gate = flat(tiles[u]["gate"][:, half, :])
-            engine = nc.vector if (u, half.start // 2) in V_SPLIT else nc.gpsimd
-            engine.tensor_tensor(out=gate, in0=gate, in1=flat(tiles[u]["m_new"][:, half, :]), op=ALU.subtract)
+            t = tiles[u]
+            gate = flat(t["gate"][:, half.start : half.stop, :])
+            m_new = flat(t["m_new"][:, half.start : half.stop, :])
+            nc.gpsimd.tensor_tensor(out=gate, in0=gate, in1=m_new, op=ALU.subtract)
 
-        def exp_and_store(u, name, scale, tensor, half, late_stores):
-            part = tiles[u][name][:, half, :]
+        def final_exp(u, name, half):
+            part = tiles[u][name][:, half.start : half.stop, :]
+            scale, tensor = {"over": (-1.0, out_2), "gate": (1.0, out_1)}[name]
             nc.scalar.activation(out=flat(part), in_=flat(part), func=ACT.Exp, scale=scale)
-            if late_stores is None:
-                nc.sync.dma_start(out=unit_view(tensor, u)[:, half, :], in_=part)
-            else:
-                late_stores.append((unit_view(tensor, u)[:, half, :], part))
+            return half_view(tensor, u, half), part
 
-        def forget_final(u, half, late_stores=None):
-            exp_and_store(u, "over", -1.0, out_2, half, late_stores)
+        def store(finished):
+            target, part = finished
+            nc.sync.dma_start(out=target, in_=part)
 
-        def input_final(u, half, late_stores=None):
-            exp_and_store(u, "gate", 1.0, out_1, half, late_stores)
-
-        def load_bf():
-            nc.sync.dma_start(out=bf_rows[0:OUT_CHUNKS, :], in_=b_f.rearrange("(c n) -> c n", c=OUT_CHUNKS))
-
-        for what in HEAD:
-            if what == "0":
-                load_activations(0, halves if HALVED > 0 else (whole,))
-            if what == "1":
-                load_activations(1, halves if HALVED > 1 else (whole,))
-            if what == "x":
-                load_weight("f_x")
-            if what == "h":
-                load_weight("f_h")
-            if what == "b":
-                load_bf()
-            if what == "p":
-                load_activations(1, names=("x",))
-            if what == "q":
-                load_activations(1, names=("h",))
-        def load_input_gate():
-            nc.sync.dma_start(out=bi_row[0:1, :], in_=b_i.rearrange("(o n) -> o n", o=1))
-            load_weight("i_x")
-            load_weight("i_h")
-
-        for u in range(2, LOADED):
-            if I_AT == u:
-                load_input_gate()
+        load_activations(0)
+        nc.sync.dma_start(out=bf_rows[0:OUT_CHUNKS, :], in_=b_f.rearrange("(c n) -> c n", c=OUT_CHUNKS))
+        load_activations(1)
+        load_weight("f_x")
+        load_weight("f_h")
+        for u in range(2, LOAD_BUFS):
             load_activations(u)
-        if I_AT == LOADED:
-            load_input_gate()
+        nc.sync.dma_start(out=bi_row[0:1, :], in_=b_i.rearrange("(o n) -> o n", o=1))
+        load_weight("i_x")
+        load_weight("i_h")
         load_m_prev(0)
 
-        neg_bf = keep.tile([P, OUT_CHUNKS], F32, name="neg_bf")
-        bias_i = keep.tile([P, FEAT], F32, name="bias_i")
-        if HALVED > 0:
-            transpose_in(0, pairs=(0,))
-            transpose_in(0, pairs=(1,))
-        else:
-            transpose_in(0)
+        transpose_in(0)
         bf_T = sbanks.tile([P, P], BF16, name="bf_T", tag="sbank")
         nc.tensor.transpose(out=bf_T[:], in_=bf_rows[:], identity=ident_bf16[:])
         nc.vector.tensor_scalar_mul(out=neg_bf[:], in0=bf_T[:, 0:OUT_CHUNKS], scalar1=-1.0)
-
-        quantise(0, "x")
-        quantise(0, "h")
-        if HALVED > 1:
-            transpose_in(1, pairs=(0,))
-            transpose_in(1, pairs=(1,))
-        else:
-            transpose_in(1)
+        quantise(0)
+        transpose_in(1)
         forget_gate(0)
-        quantise(1, "x")
-        quantise(1, "h")
-        ln_done = 0
-        ln_done = 0
-        diff_step = {}
-        step = 0
-        first = 0
-        for end in RUN_ENDS:
-            step = max(step, end + 1)
-            for u in range(first, end + 1):
-                diff_step[step] = u
-                step += 1
-            first = end + 1
-        fin_wait = []
-        m_order = sorted(diff_step)
-        for s in range(step + 1):
-            middle = diff_step.get(s, -1)
-            for u, step_of_load in LOAD_AT:
-                if step_of_load == s:
-                    load_activations(u)
-            for key in m_order:
-                if key <= s + M_AHEAD and diff_step[key] not in m_tiles:
-                    load_m_prev(diff_step[key])
+        quantise(1)
+
+        for s in range(N_UNITS + LAG):
+            coming = s + 2
+            middle = s - LAG
+            last = middle - 1
+            behind_log = s % RUN == 0 and s > 0
+            with_log = s % RUN == RUN - 1 and s < N_UNITS
+
+            if s + LOAD_BUFS < N_UNITS:
+                load_activations(s + LOAD_BUFS)
+            if s + 1 < N_UNITS:
+                load_m_prev(s + 1)
             if s < N_UNITS:
                 forget_exp(s)
-            late_stores = [] if s - 1 in POST else None
-            deferred = []
-            for u, half in fin_wait:
-                if s in DEFER and half == halves[1]:
-                    deferred.append((u, half))
-                else:
-                    input_exponent(u, half)
-            if fin_wait:
-                u = fin_wait[0][0]
-                for half in halves:
-                    forget_final(u, half, late_stores)
-                for u, half in fin_wait:
-                    if (u, half) not in deferred:
-                        input_final(u, half, late_stores)
-            fin_wait = []
+
+            stores = []
+            deferred = None
+            if 0 <= last < LATE:
+                deferred = HALVES[1] if last == 0 else None
+                prompt = [half for half in HALVES if half is not deferred]
+                for half in prompt:
+                    input_exponent(last, half)
+                work = [("over", half) for half in HALVES] + [("gate", half) for half in prompt]
+                for name, half in work:
+                    finished = final_exp(last, name, half)
+                    if last == LATE - 1:
+                        stores.append(finished)
+                    else:
+                        store(finished)
             if s < N_UNITS:
                 clamp(s)
-            for u, half in deferred:
-                input_exponent(u, half)
+            if deferred is not None:
+                input_exponent(last, deferred)
             if middle == 0:
-                bi_sum = vbanks.tile([P, FEAT], F32, name="bi_sum", tag="vbank")
-                nc.tensor.matmul(out=bi_sum[:], lhsT=ones[:], rhs=bi_row[:], start=True, stop=True)
-                nc.vector.tensor_copy(out=bias_i[:], in_=bi_sum[:])
-            for work in ORDER.get(s, "AIDQF"):
-                if work == "A" and 2 <= s + AH < N_UNITS:
-                    transpose_in(s + AH)
-                if work == "I" and middle >= 0 and "gate" not in tiles[middle]:
-                    input_gate(middle)
-                if work == "D" and middle >= 0:
-                    for half in halves:
-                        new_maximum(middle, range(half.start, half.stop))
-                        if s in WEAVE:
-                            for target, part in late_stores[:2]:
-                                nc.sync.dma_start(out=target, in_=part)
-                            late_stores = late_stores[2:]
-                if work == "Q" and 2 <= s + AH < N_UNITS:
-                    quantise(s + AH, "x")
-                    quantise(s + AH, "h")
-                if work == "F" and s + 1 < N_UNITS:
-                    forget_gate(s + 1)
-            for target, part in late_stores or ():
-                nc.sync.dma_start(out=target, in_=part)
-            if middle >= 0:
-                for half in halves:
-                    if middle >= LATE or (middle == HALF_LATE and half == halves[0]):
-                        input_exponent(middle, half)
-                        forget_final(middle, half)
-                        input_final(middle, half)
-                    else:
-                        fin_wait.append((middle, half))
-            for u in EARLY_I.get(s, ()):
-                input_gate(u)
-            if s in RUN_ENDS:
-                for u in range(ln_done, s + 1):
+                spread_b_i()
+
+            if s == 0:
+                order = (transpose_in, forget_gate, quantise)
+            elif behind_log:
+                order = (input_gate, new_maximum, forget_gate, transpose_in, quantise)
+            else:
+                order = (input_gate, transpose_in, new_maximum, quantise, forget_gate)
+            unit_of = {
+                transpose_in: coming,
+                quantise: coming,
+                forget_gate: s + 1,
+                input_gate: middle,
+                new_maximum: middle,
+            }
+            for stage in order:
+                if 0 <= unit_of[stage] < N_UNITS:
+                    stage(unit_of[stage])
+
+            for finished in stores:
+                store(finished)
+            if middle >= LATE:
+                for half in HALVES:
+                    input_exponent(middle, half)
+                    store(final_exp(middle, "over", half))
+                    store(final_exp(middle, "gate", half))
+            if with_log:
+                for u in range(s - RUN + 1, s + 1):
                     log(u)
-                ln_done = s + 1
-            for u, half in deferred:
-                input_final(u, half, None)
+            if deferred is not None:
+                store(final_exp(last, "gate", deferred))

from contextlib import ExitStack

import concourse.mybir as mybir
from concourse.masks import make_identity

F32 = mybir.dt.float32
BF16 = mybir.dt.bfloat16
I32 = mybir.dt.int32
U32 = mybir.dt.uint32
U8 = mybir.dt.uint8
FP8X4 = mybir.dt.float8_e4m3fn_x4
FP4X4 = mybir.dt.float4_e2m1fn_x4
ALU = mybir.AluOpType
ACT = mybir.ActivationFunctionType

P = 128
BATCH = 4096
FEAT = 512
ROW_TILES = 4
UNIT_ROWS = P * ROW_TILES
N_UNITS = BATCH // UNIT_ROWS
OUT_CHUNKS = FEAT // P
WORDS = FEAT // 2
QUADRANTS = 4
HALVES = (range(0, ROW_TILES // 2), range(ROW_TILES // 2, ROW_TILES))

RUN = 2
LAG = 2
LATE = N_UNITS - RUN

LOAD_BUFS = 4
M_BUFS = 4
QUANT_BUFS = 6
SOFT_BUFS = 4
GATE_BUFS = 4
SHORT_BUFS = 3
VBANKS = 4

FLOPS = 2 * BATCH * FEAT * FEAT * 4


def tile_slstmlayer_pa_t_kernel(
    tc,
    x,
    h_prev,
    m_prev,
    Wi_x_words,
    Wi_x_scales,
    b_i,
    Wi_h_words,
    Wi_h_scales,
    Wf_x_words,
    Wf_x_scales,
    b_f,
    Wf_h_words,
    Wf_h_scales,
    out_0,
    out_1,
    out_2,
):
    nc = tc.nc
    with ExitStack() as stack:
        keep = stack.enter_context(tc.tile_pool(name="keep", bufs=1))
        loads = stack.enter_context(tc.tile_pool(name="loads", bufs=LOAD_BUFS))
        m_pool = stack.enter_context(tc.tile_pool(name="m_pool", bufs=M_BUFS))
        regroup = stack.enter_context(tc.tile_pool(name="regroup", bufs=2))
        quant = stack.enter_context(tc.tile_pool(name="quant", bufs=QUANT_BUFS))
        soft_pool = stack.enter_context(tc.tile_pool(name="soft_pool", bufs=SOFT_BUFS))
        gate_pool = stack.enter_context(tc.tile_pool(name="gate_pool", bufs=GATE_BUFS))
        short = stack.enter_context(tc.tile_pool(name="short", bufs=SHORT_BUFS))
        vbanks = stack.enter_context(tc.psum_pool(name="vbanks", bufs=VBANKS))
        sbanks = stack.enter_context(tc.psum_pool(name="sbanks", bufs=8 - VBANKS))
        stack.enter_context(tc.manual_schedule())

        def unit_view(tensor, u):
            rows = tensor[u * UNIT_ROWS : (u + 1) * UNIT_ROWS, :]
            return rows.rearrange("(p j) n -> p j n", j=ROW_TILES)

        def half_view(tensor, u, half):
            return unit_view(tensor, u)[:, half.start : half.stop, :]

        ident_f32 = keep.tile([P, P], F32, name="ident_f32")
        make_identity(nc, ident_f32[:])
        ident_bf16 = keep.tile([P, P], BF16, name="ident_bf16")
        make_identity(nc, ident_bf16[:])

        weight_names = ("f_x", "f_h", "i_x", "i_h")
        weight_words = {"f_x": Wf_x_words, "f_h": Wf_h_words, "i_x": Wi_x_words, "i_h": Wi_h_words}
        weight_scales = {"f_x": Wf_x_scales, "f_h": Wf_h_scales, "i_x": Wi_x_scales, "i_h": Wi_h_scales}
        ones = keep.tile([P, P], BF16, name="ones")
        nc.vector.memset(ones[:], 1.0)
        bi_row = keep.tile([P, FEAT], BF16, name="bi_row")
        nc.vector.memset(bi_row[:], 0.0)
        planes = keep.tile([P, len(weight_names), FEAT], U8, name="planes", align_bytes=64)
        nc.vector.memset(planes[:].rearrange("p w n -> p (w n)").bitcast(I32), 0)
        bf_rows = keep.tile([P, P], BF16, name="bf_rows")
        nc.vector.memset(bf_rows[:], 0.0)
        one_column = keep.tile([P, 1], F32, name="one_column")
        nc.vector.memset(one_column[:], 0.0)
        nc.scalar.activation(out=one_column[:], in_=one_column[:], func=ACT.Exp)
        neg_ident = keep.tile([P, P], BF16, name="neg_ident")
        nc.vector.tensor_scalar_mul(out=neg_ident[:], in0=ident_bf16[:], scalar1=-1.0)
        neg_bf = keep.tile([P, OUT_CHUNKS], F32, name="neg_bf")
        bias_i = keep.tile([P, FEAT], F32, name="bias_i")

        words = {}

        def load_weight(w):
            words[w] = keep.tile([P, 2 * FEAT], U8, name="words_" + w, align_bytes=64)
            nc.sync.dma_start(
                out=words[w][:].bitcast(I32),
                in_=weight_words[w].rearrange("g p b -> (g p) b").bitcast(I32),
            )
            scale_rows = weight_scales[w].rearrange("g q n -> (g q) n")
            for quad in range(QUADRANTS):
                nc.sync.dma_start(
                    out=planes[32 * quad : 32 * quad + 4, weight_names.index(w), :].bitcast(I32),
                    in_=scale_rows[4 * quad : 4 * quad + 4, :].bitcast(I32),
                )

        def weight_plane(w):
            return planes[:, weight_names.index(w), :]

        tiles = {u: {} for u in range(N_UNITS)}

        def load_activations(u):
            for name, tensor in (("x", x), ("h", h_prev)):
                rows = loads.tile([P, ROW_TILES, FEAT], BF16, name=name + "_rows")
                nc.sync.dma_start(out=rows[:], in_=unit_view(tensor, u))
                tiles[u][name] = rows

        def load_m_prev(u):
            rows = m_pool.tile([P, ROW_TILES, FEAT], BF16, name="m_rows")
            nc.sync.dma_start(out=rows[:], in_=unit_view(m_prev, u))
            tiles[u]["m"] = rows

        def flat(view):
            return view.rearrange("p j n -> p (j n)")

        def transpose_in(u):
            for name in ("x", "h"):
                row_words = tiles[u][name][:].rearrange("p j k -> p (j k)").bitcast(F32)
                grouped = regroup.tile([P, 4 * UNIT_ROWS], BF16, name=name + "_grouped", align_bytes=64)
                grouped_words = grouped[:].bitcast(F32).rearrange("p (c v) -> p c v", v=2)
                for pair in range(ROW_TILES // 2):
                    bank = vbanks.tile([P, 2, 2, P], F32, name="words_T", tag="vbank")
                    for jj in range(2):
                        first = (2 * pair + jj) * WORDS
                        for v in range(2):
                            nc.tensor.transpose(
                                out=bank[:, jj, v, :],
                                in_=row_words[:, first + v : first + WORDS : 2],
                                identity=ident_f32[:],
                            )
                    target = grouped_words[:, 2 * pair * P : (2 * pair + 2) * P, :].rearrange(
                        "p (jj r) v -> p jj r v", jj=2
                    )
                    nc.vector.tensor_copy(out=target, in_=bank[:].rearrange("p jj v r -> p jj r v"))
                tiles[u][name + "_grouped"] = grouped

        def quantise(u):
            for name in ("x", "h"):
                codes = quant.tile([P, UNIT_ROWS], U32, name=name + "_codes", align_bytes=64)
                scales = quant.tile([P, UNIT_ROWS], U8, name=name + "_scales", align_bytes=64)
                nc.vector.quantize_mx(
                    out=codes[:].bitcast(FP8X4), scales=scales[:], in_=tiles[u][name + "_grouped"][:]
                )
                tiles[u][name + "_codes"] = codes
                tiles[u][name + "_scales"] = scales

        def forget_gate(u):
            t = tiles[u]
            passes = [(c, name) for c in range(OUT_CHUNKS) for name in ("x", "h")]
            if u == 0:
                passes = [(c, name) for name in ("x", "h") for c in range(OUT_CHUNKS)]
            t["f_T"] = {}
            for c, name in passes:
                if name == "x":
                    acc = sbanks.tile([P, UNIT_ROWS], F32, name="f_T", tag="sbank")
                    t["f_T"][c] = acc
                nc.tensor.matmul_mx(
                    out=t["f_T"][c][:],
                    lhsT=words["f_" + name][:, 2 * c * P : 2 * (c + 1) * P].bitcast(FP4X4),
                    lhsT_scale=weight_plane("f_" + name)[:, c * P : (c + 1) * P],
                    rhs=t[name + "_codes"][:].bitcast(FP8X4),
                    rhs_scale=t[name + "_scales"][:],
                    start=(name == "x"),
                    stop=(name == "h"),
                )

        def forget_exp(u):
            t = tiles[u]
            soft = soft_pool.tile([P, OUT_CHUNKS, UNIT_ROWS], F32, name="soft_T")
            for c in range(OUT_CHUNKS):
                nc.scalar.activation(
                    out=soft[:, c, :], in_=t["f_T"][c][:], func=ACT.Exp, bias=neg_bf[:, c : c + 1], scale=-1.0
                )
            t["soft_T"] = soft

        def clamp(u):
            for c in range(0, OUT_CHUNKS, 2):
                part = flat(tiles[u]["soft_T"][:, c : c + 2, :])
                nc.gpsimd.tensor_scalar(
                    out=part, in0=part, scalar1=1.0e8 - 1.0, scalar2=0.0, op0=ALU.min, op1=ALU.max
                )

        def log(u):
            soft = tiles[u]["soft_T"]
            for half in HALVES:
                part = soft[:, :, half.start * P : half.stop * P]
                nc.scalar.activation(out=part, in_=part, func=ACT.Ln, bias=1.0)

        def spread_b_i():
            bi_sum = vbanks.tile([P, FEAT], F32, name="bi_sum", tag="vbank")
            nc.tensor.matmul(out=bi_sum[:], lhsT=ones[:], rhs=bi_row[:], start=True, stop=True)
            nc.vector.tensor_copy(out=bias_i[:], in_=bi_sum[:])

        def input_gate(u):
            t = tiles[u]
            gate = gate_pool.tile([P, ROW_TILES, FEAT], F32, name="gate")
            for j in range(ROW_TILES):
                acc = vbanks.tile([P, FEAT], F32, name="i_rows", tag="vbank")
                for name in ("x", "h"):
                    nc.tensor.matmul_mx(
                        out=acc[:],
                        lhsT=t[name + "_codes"][:, j * P : (j + 1) * P].bitcast(FP8X4),
                        lhsT_scale=t[name + "_scales"][:, j * P : (j + 1) * P],
                        rhs=words["i_" + name][:].bitcast(FP4X4),
                        rhs_scale=weight_plane("i_" + name),
                        start=(name == "x"),
                        stop=(name == "h"),
                    )
                nc.vector.tensor_tensor(out=gate[:, j, :], in0=acc[:], in1=bias_i[:], op=ALU.add)
            t["gate"] = gate

        def new_maximum(u):
            t = tiles[u]
            m_new = short.tile([P, ROW_TILES, FEAT], F32, name="m_new")
            over = short.tile([P, ROW_TILES, FEAT], F32, name="over")
            for half in HALVES:
                banks = {}
                for j in half:
                    bank = vbanks.tile([P, FEAT], F32, name="s_minus_m", tag="vbank")
                    nc.tensor.matmul(out=bank[:], lhsT=neg_ident[:], rhs=t["m"][:, j, :], start=True, stop=False)
                    banks[j] = bank
                for j in half:
                    for c in range(OUT_CHUNKS):
                        nc.tensor.matmul(
                            out=banks[j][:, c * P : (c + 1) * P],
                            lhsT=t["soft_T"][:, c, j * P : (j + 1) * P],
                            rhs=ident_f32[:],
                            is_transpose=True,
                            start=False,
                            stop=(c == OUT_CHUNKS - 1),
                        )
                    nc.vector.scalar_tensor_tensor(
                        out=m_new[:, j, :],
                        in0=banks[j][:],
                        scalar=-1.0,
                        in1=t["gate"][:, j, :],
                        op0=ALU.mult,
                        op1=ALU.max,
                    )
                nc.sync.dma_start(out=half_view(out_0, u, half), in_=m_new[:, half.start : half.stop, :])
                for j in half:
                    nc.vector.tensor_tensor(out=over[:, j, :], in0=banks[j][:], in1=m_new[:, j, :], op=ALU.add)
            t["m_new"] = m_new
            t["over"] = over

        def input_exponent(u, half):
            t = tiles[u]
            gate = flat(t["gate"][:, half.start : half.stop, :])
            m_new = flat(t["m_new"][:, half.start : half.stop, :])
            nc.gpsimd.tensor_tensor(out=gate, in0=gate, in1=m_new, op=ALU.subtract)

        def final_exp(u, name, half):
            part = tiles[u][name][:, half.start : half.stop, :]
            scale, tensor = {"over": (-1.0, out_2), "gate": (1.0, out_1)}[name]
            nc.scalar.activation(out=flat(part), in_=flat(part), func=ACT.Exp, scale=scale)
            return half_view(tensor, u, half), part

        def store(finished):
            target, part = finished
            nc.sync.dma_start(out=target, in_=part)

        load_activations(0)
        nc.sync.dma_start(out=bf_rows[0:OUT_CHUNKS, :], in_=b_f.rearrange("(c n) -> c n", c=OUT_CHUNKS))
        load_activations(1)
        load_weight("f_x")
        load_weight("f_h")
        for u in range(2, LOAD_BUFS):
            load_activations(u)
        nc.sync.dma_start(out=bi_row[0:1, :], in_=b_i.rearrange("(o n) -> o n", o=1))
        load_weight("i_x")
        load_weight("i_h")
        load_m_prev(0)

        transpose_in(0)
        bf_T = sbanks.tile([P, P], BF16, name="bf_T", tag="sbank")
        nc.tensor.transpose(out=bf_T[:], in_=bf_rows[:], identity=ident_bf16[:])
        nc.vector.tensor_scalar_mul(out=neg_bf[:], in0=bf_T[:, 0:OUT_CHUNKS], scalar1=-1.0)
        quantise(0)
        transpose_in(1)
        forget_gate(0)
        quantise(1)

        for s in range(N_UNITS + LAG):
            coming = s + 2
            middle = s - LAG
            last = middle - 1
            behind_log = s % RUN == 0 and s > 0
            with_log = s % RUN == RUN - 1 and s < N_UNITS

            if s + LOAD_BUFS < N_UNITS:
                load_activations(s + LOAD_BUFS)
            if s + 1 < N_UNITS:
                load_m_prev(s + 1)
            if s < N_UNITS:
                forget_exp(s)

            stores = []
            deferred = None
            if 0 <= last < LATE:
                deferred = HALVES[1] if last == 0 else None
                prompt = [half for half in HALVES if half is not deferred]
                for half in prompt:
                    input_exponent(last, half)
                work = [("over", half) for half in HALVES] + [("gate", half) for half in prompt]
                for name, half in work:
                    finished = final_exp(last, name, half)
                    if last == LATE - 1:
                        stores.append(finished)
                    else:
                        store(finished)
            if s < N_UNITS:
                clamp(s)
            if deferred is not None:
                input_exponent(last, deferred)
            if middle == 0:
                spread_b_i()

            if s == 0:
                order = (transpose_in, forget_gate, quantise)
            elif behind_log:
                order = (input_gate, new_maximum, forget_gate, transpose_in, quantise)
            else:
                order = (input_gate, transpose_in, new_maximum, quantise, forget_gate)
            unit_of = {
                transpose_in: coming,
                quantise: coming,
                forget_gate: s + 1,
                input_gate: middle,
                new_maximum: middle,
            }
            for stage in order:
                if 0 <= unit_of[stage] < N_UNITS:
                    stage(unit_of[stage])

            for finished in stores:
                store(finished)
            if middle >= LATE:
                for half in HALVES:
                    input_exponent(middle, half)
                    store(final_exp(middle, "over", half))
                    store(final_exp(middle, "gate", half))
            if with_log:
                for u in range(s - RUN + 1, s + 1):
                    log(u)
            if deferred is not None:
                store(final_exp(last, "gate", deferred))
